import numpy as np
import ml_dtypes


def mxq(x, axis, fmt="e4m3"):
    dtype, down = {"e4m3": (ml_dtypes.float8_e4m3fn, 7), "e5m2": (ml_dtypes.float8_e5m2, 14)}[fmt]
    v = np.moveaxis(np.asarray(x, np.float32).astype(ml_dtypes.bfloat16).astype(np.float64), axis, -1)
    blocks = v.reshape(v.shape[:-1] + (-1, 32))
    amax = np.abs(blocks).max(-1, keepdims=True)
    byte = np.maximum(np.where(amax > 0, np.frexp(amax)[1] - 1 + 127, 0) - down, 1)
    scale = np.exp2(byte - 127.0)
    codes = (blocks / scale).astype(np.float32).astype(dtype).astype(np.float64)
    return np.moveaxis((codes * scale).reshape(v.shape), -1, axis)


WIDE = False


def mx_kscale(k):
    if not WIDE:
        return np.ones(k)
    levels = np.array([10, -10, 5, -5, 0])
    a = np.random.permutation(np.resize(levels, k // 512 * 4)).reshape(k // 512, 4)
    idx = np.arange(k)
    return np.exp2(a[idx // 512, idx % 128 // 32])


BF16 = ml_dtypes.bfloat16


def bf(x):
    return np.asarray(x, np.float32).astype(BF16)


def f64(x):
    return np.asarray(x).astype(np.float64)


B, N, F_NODE, F_EDGE, H = 8, 16, 64, 32, 1024


def setup_inputs():
    s, t = mx_kscale(H), mx_kscale(H)
    w1 = np.random.standard_normal((3 * H, H)) / np.sqrt(3 * H) * t
    w1[2 * H:] = w1[2 * H:] / s[:, None]
    return {"h": bf(np.random.standard_normal((B, N, H))),
            "e": bf(np.random.standard_normal((B, N, N, H)) * s),
            "adj_mask": bf(np.random.uniform(size=(B, N, N, 1)) < 0.5),
            "W_m1": bf(w1),
            "b_m1": bf(np.random.standard_normal(H) * 0.3 * t),
            "W_m2": bf(np.random.standard_normal((H, H)) * 2.0 / np.sqrt(H * N) / t[:, None]),
            "b_m2": bf(np.random.standard_normal(H) * 0.4 / np.sqrt(N))}


def reference(h, e, adj_mask, W_m1, b_m1, W_m2, b_m2):
    h = f64(h)
    w1 = f64(W_m1)
    hq = mxq(h, 2, "e4m3")
    a_i = hq @ mxq(w1[:H], 0, "e4m3")
    a_j = hq @ mxq(w1[H:2 * H], 0, "e4m3")
    a_e = mxq(f64(e), 3, "e4m3") @ mxq(w1[2 * H:], 0, "e4m3")
    m = a_i[:, :, None, :] + a_j[:, None, :, :] + a_e + f64(b_m1)
    m = np.maximum(m, 0.0)
    m = (mxq(m, 3, "e4m3") @ mxq(f64(W_m2), 0, "e4m3")) + f64(b_m2)
    m = m * f64(adj_mask)
    return m.sum(axis=-2) + h

@@ -1,0 +1,318 @@
+from contextlib import ExitStack
+
+import concourse.mybir as mybir
+from concourse.masks import make_identity
+
+FP8X4 = mybir.dt.float8_e4m3fn_x4
+BF16 = mybir.dt.bfloat16
+F32 = mybir.dt.float32
+U32 = mybir.dt.uint32
+U8 = mybir.dt.uint8
+ADD = mybir.AluOpType.add
+MULT = mybir.AluOpType.mult
+RELU = mybir.ActivationFunctionType.Relu
+
+P = 128
+PACK = 4
+K_PASS = P * PACK
+BANK = 512
+GRAPHS = 8
+GRAPH_NODES = 16
+NODES = GRAPHS * GRAPH_NODES
+WIDTH = 1024
+EDGES = NODES * GRAPH_NODES
+PASSES = WIDTH // K_PASS
+BLOCKS = WIDTH // P
+J_TILE = BANK // NODES
+COL_TILES = GRAPH_NODES // J_TILE
+HALVES = WIDTH // BANK
+RUN = 4
+
+XI_CHUNK, XJ_CHUNK, E2_CHUNK, M2_CHUNK = 0, 2, 4, 6
+WEIGHT_CHUNKS = 8
+W1_VECTOR_COLS = WIDTH // 2
+
+FLOPS = 2 * WIDTH * WIDTH * (2 * NODES + 2 * EDGES)
+
+
+def tile_messagepassing_pa_kernel(tc, h, e, adj_mask, W_m1, b_m1, W_m2, b_m2, out):
+    nc = tc.nc
+    h_rows = h.rearrange("b i k -> (b i) k")
+    e_rows = e.rearrange("b i j k -> (b i) j k")
+    mask_rows = adj_mask.rearrange("b i j o -> (b i) (j o)")
+    out_rows = out.rearrange("b i f -> (b i) f")
+
+    with ExitStack() as stack:
+        keep = stack.enter_context(tc.tile_pool(name="keep", bufs=1))
+        raw_pool = stack.enter_context(tc.tile_pool(name="raw", bufs=4))
+        edge_pool = stack.enter_context(tc.tile_pool(name="edge", bufs=3))
+        grouped_pool = stack.enter_context(tc.tile_pool(name="grouped", bufs=2))
+        stage = stack.enter_context(tc.tile_pool(name="stage", bufs=2))
+        pair_pool = stack.enter_context(tc.tile_pool(name="pair", bufs=2 * PACK))
+        psum = stack.enter_context(tc.psum_pool(name="psum", bufs=2))
+
+        b1_rows = keep.tile([P, P], BF16)
+        nc.vector.memset(b1_rows[:], 0.0)
+        nc.scalar.dma_start(out=b1_rows[0:BLOCKS, :], in_=b_m1.rearrange("(m p) -> m p", p=P))
+        mask_bf16 = keep.tile([P, GRAPH_NODES], BF16)
+        nc.scalar.dma_start(out=mask_bf16[:], in_=mask_rows)
+        b2_row = keep.tile([P, WIDTH], BF16)
+        nc.gpsimd.memset(b2_row[:], 0.0)
+        nc.scalar.dma_start(out=b2_row[0:1, :], in_=b_m2.rearrange("(o f) -> o f", o=1))
+
+        h_sb = keep.tile([P, WIDTH], BF16)
+        nc.sync.dma_start(out=h_sb[:], in_=h_rows)
+
+        def load_w1_chunk(chunk):
+            raw = raw_pool.tile([P, PACK, WIDTH], BF16, name="raw", tag="raw")
+            rows = W_m1[chunk * K_PASS : (chunk + 1) * K_PASS, :]
+            nc.sync.dma_start(
+                out=raw[:].rearrange("p (u s) n -> p u s n", u=2),
+                in_=rows.rearrange("(u p s) n -> p u s n", u=2, s=2),
+            )
+            return raw
+
+        def load_w2_chunk(g):
+            raw = raw_pool.tile([P, PACK, WIDTH], BF16, name="raw", tag="raw")
+            rows = W_m2[g * K_PASS : (g + 1) * K_PASS, :]
+            nc.sync.dma_start(out=raw[:], in_=rows.rearrange("(t p) n -> p t n", t=PACK))
+            return raw
+
+        def load_edges(c):
+            e_sb = edge_pool.tile([P, J_TILE, WIDTH], BF16, name="e_sb", tag="e_sb")
+            nc.sync.dma_start(out=e_sb[:], in_=e_rows[:, c * J_TILE : (c + 1) * J_TILE, :])
+            return e_sb
+
+        raw_chunks = [load_w1_chunk(chunk) for chunk in range(M2_CHUNK)]
+        e_tiles = [load_edges(0)]
+        raw_chunks.extend([load_w2_chunk(g) for g in range(PASSES)])
+        e_tiles.extend([load_edges(c) for c in range(1, COL_TILES)])
+
+        ident_f32 = keep.tile([P, P], F32)
+        make_identity(nc, ident_f32[:])
+        ident_bf16 = keep.tile([P, P], BF16)
+        make_identity(nc, ident_bf16[:])
+        ones = keep.tile([P, P], BF16)
+        nc.vector.memset(ones[:], 1.0)
+
+        w_codes = keep.tile([P, WEIGHT_CHUNKS, WIDTH], U32, align_bytes=64)
+        w_scales = keep.tile([P, WEIGHT_CHUNKS, WIDTH], U8, align_bytes=64)
+        h_codes = keep.tile([P, PASSES, NODES], U32, align_bytes=64)
+        h_scales = keep.tile([P, PASSES, NODES], U8, align_bytes=64)
+        e_codes = keep.tile([P, PASSES, EDGES], U32, align_bytes=64)
+        e_scales = keep.tile([P, PASSES, EDGES], U8, align_bytes=64)
+        r_codes = keep.tile([P, PASSES, EDGES], U32, align_bytes=64)
+        r_scales = keep.tile([P, PASSES, EDGES], U8, align_bytes=64)
+
+        def regroup(copy, grouped, raw, cols):
+            copy(
+                out=grouped[:, cols, :].rearrange("p (c i) t -> p c t i", i=RUN),
+                in_=raw[:, :, cols].rearrange("p t (c i) -> p c t i", i=RUN),
+            )
+
+        def quantise_weights(chunk, vector_cols):
+            raw = raw_chunks[chunk]
+            grouped = grouped_pool.tile([P, WIDTH, PACK], BF16, name="grouped", tag="grouped", align_bytes=64)
+            if vector_cols > 0:
+                regroup(nc.vector.tensor_copy, grouped, raw, slice(0, vector_cols))
+            regroup(nc.scalar.copy, grouped, raw, slice(vector_cols, WIDTH))
+            nc.vector.quantize_mx(
+                out=w_codes[:, chunk, :].bitcast(FP8X4),
+                scales=w_scales[:, chunk, :],
+                in_=grouped[:].rearrange("p n t -> p (n t)"),
+            )
+
+        def transpose_words(bank_cols, rows_bf16, g, u):
+            first = (K_PASS * g + 2 * P * u) // 2
+            nc.tensor.transpose(bank_cols, rows_bf16.bitcast(F32)[:, first : first + P], ident_f32[:])
+
+        h_bank = psum.tile([P, PASSES, 2, NODES], F32, name="h_bank", tag="small")
+        for g in range(PASSES):
+            for u in range(2):
+                transpose_words(h_bank[:, g, u, :], h_sb[:], g, u)
+        h_grouped = keep.tile([P, PASSES * NODES * PACK], BF16, align_bytes=64)
+        nc.vector.tensor_copy(
+            out=h_grouped[:].bitcast(F32).rearrange("p (g n u) -> p g n u", g=PASSES, u=2),
+            in_=h_bank[:].rearrange("p g u n -> p g n u"),
+        )
+        nc.vector.quantize_mx(
+            out=h_codes[:].rearrange("p g n -> p (g n)").bitcast(FP8X4),
+            scales=h_scales[:].rearrange("p g n -> p (g n)"),
+            in_=h_grouped[:],
+        )
+
+        b1_bank = psum.tile([P, P], BF16, name="b1_bank", tag="small")
+        nc.tensor.transpose(b1_bank[:], b1_rows[:], ident_bf16[:])
+        b1 = keep.tile([P, BLOCKS], F32)
+        nc.vector.tensor_copy(out=b1[:], in_=b1_bank[:, 0:BLOCKS])
+
+        mask = keep.tile([P, GRAPH_NODES], F32)
+        nc.vector.tensor_copy(out=mask[:], in_=mask_bf16[:])
+        mask_sum = keep.tile([P, 1], F32)
+        nc.vector.tensor_reduce(out=mask_sum[:], in_=mask[:], axis=mybir.AxisListType.X, op=ADD)
+
+        acc = keep.tile([P, WIDTH], F32)
+        for f in range(HALVES):
+            feats = slice(f * BANK, (f + 1) * BANK)
+            b2_bank = psum.tile([P, BANK], F32, name="b2_bank", tag="small")
+            nc.tensor.matmul(out=b2_bank[:], lhsT=ones[:], rhs=b2_row[:, feats], start=True, stop=True)
+            nc.vector.scalar_tensor_tensor(
+                out=acc[:, feats], in0=b2_bank[:], scalar=mask_sum[:, 0:1], in1=h_sb[:, feats], op0=MULT, op1=ADD
+            )
+
+        def node_term_bank(first_chunk, half):
+            bank = psum.tile([P, PACK, NODES], F32, name="node_bank", tag="small")
+            for t in range(PACK):
+                units = slice((PACK * half + t) * P, (PACK * half + t + 1) * P)
+                for kp in range(PASSES):
+                    nc.tensor.matmul_mx(
+                        out=bank[:, t, :],
+                        lhsT=w_codes[:, first_chunk + kp, units].bitcast(FP8X4),
+                        lhsT_scale=w_scales[:, first_chunk + kp, units],
+                        rhs=h_codes[:, kp, :].bitcast(FP8X4),
+                        rhs_scale=h_scales[:, kp, :],
+                        start=(kp == 0),
+                        stop=(kp == PASSES - 1),
+                    )
+            return bank
+
+        target_term = keep.tile([P, BLOCKS, NODES], F32)
+        source_term = keep.tile([P, BLOCKS, NODES], F32)
+
+        for chunk in range(XI_CHUNK, XI_CHUNK + PASSES):
+            quantise_weights(chunk, W1_VECTOR_COLS)
+        for half in range(BLOCKS // PACK):
+            blocks = slice(PACK * half, PACK * (half + 1))
+            bank = node_term_bank(XI_CHUNK, half)
+            nc.vector.tensor_tensor(
+                out=target_term[:, blocks, :],
+                in0=bank[:],
+                in1=b1[:, blocks].unsqueeze(2).to_broadcast([P, PACK, NODES]),
+                op=ADD,
+            )
+        for chunk in range(XJ_CHUNK, XJ_CHUNK + PASSES):
+            quantise_weights(chunk, W1_VECTOR_COLS)
+        for half in range(BLOCKS // PACK):
+            blocks = slice(PACK * half, PACK * (half + 1))
+            bank = node_term_bank(XJ_CHUNK, half)
+            nc.scalar.copy(out=source_term[:, blocks, :], in_=bank[:])
+
+        def pair_terms(c, g):
+            tiles = []
+            for t in range(PACK):
+                block = PACK * g + t
+                pair = pair_pool.tile([P, J_TILE, GRAPHS, GRAPH_NODES], F32, name="pair", tag="pair")
+                nc.gpsimd.tensor_tensor(
+                    out=pair[:],
+                    in0=target_term[:, block, :]
+                    .rearrange("p (b i) -> p b i", b=GRAPHS)
+                    .unsqueeze(1)
+                    .to_broadcast([P, J_TILE, GRAPHS, GRAPH_NODES]),
+                    in1=source_term[:, block, :]
+                    .rearrange("p (b j) -> p j b", b=GRAPHS)[:, c * J_TILE : (c + 1) * J_TILE, :]
+                    .unsqueeze(3)
+                    .to_broadcast([P, J_TILE, GRAPHS, GRAPH_NODES]),
+                    op=ADD,
+                )
+                tiles.append(pair)
+            return tiles
+
+        def quantise_edges(c):
+            e_sb = e_tiles[c]
+            cols = slice(c * BANK, (c + 1) * BANK)
+            for g in range(PASSES):
+                e_grouped = stage.tile([P, BANK * PACK], BF16, name="e_grouped", tag="e_grouped", align_bytes=64)
+                e_words = e_grouped[:].bitcast(F32).rearrange("p (x n u) -> p x n u", x=J_TILE, u=2)
+                for first_j in range(0, J_TILE, 2):
+                    e_bank = psum.tile([P, 2, 2, NODES], F32, name="e_bank", tag="small")
+                    for x in range(2):
+                        for u in range(2):
+                            transpose_words(e_bank[:, x, u, :], e_sb[:, first_j + x, :], g, u)
+                    nc.scalar.copy(
+                        out=e_words[:, first_j : first_j + 2, :, :],
+                        in_=e_bank[:].rearrange("p x u n -> p x n u"),
+                    )
+                nc.vector.quantize_mx(
+                    out=e_codes[:, g, cols].bitcast(FP8X4), scales=e_scales[:, g, cols], in_=e_grouped[:]
+                )
+
+        def first_layer(c, g, pairs):
+            cols = slice(c * BANK, (c + 1) * BANK)
+            p_bf16 = stage.tile([P, PACK, BANK], BF16, name="p_bf16", tag="p_bf16")
+            for t in range(PACK):
+                units = slice((PACK * g + t) * P, (PACK * g + t + 1) * P)
+                edge_bank = psum.tile([P, BANK], F32, name="edge_bank", tag="edge_bank", bufs=4)
+                for kp in range(PASSES):
+                    nc.tensor.matmul_mx(
+                        out=edge_bank[:],
+                        lhsT=w_codes[:, E2_CHUNK + kp, units].bitcast(FP8X4),
+                        lhsT_scale=w_scales[:, E2_CHUNK + kp, units],
+                        rhs=e_codes[:, kp, cols].bitcast(FP8X4),
+                        rhs_scale=e_scales[:, kp, cols],
+                        start=(kp == 0),
+                        stop=(kp == PASSES - 1),
+                    )
+                nc.vector.tensor_tensor(
+                    out=p_bf16[:, t, :],
+                    in0=edge_bank[:],
+                    in1=pairs[t][:].rearrange("p j b i -> p (j b i)"),
+                    op=ADD,
+                )
+            r_grouped = stage.tile([P, BANK, PACK], BF16, name="r_grouped", tag="r_grouped", align_bytes=64)
+            nc.scalar.activation(
+                out=r_grouped[:].rearrange("p (c i) t -> p c t i", i=RUN),
+                in_=p_bf16[:].rearrange("p t (c i) -> p c t i", i=RUN),
+                func=RELU,
+            )
+            nc.vector.quantize_mx(
+                out=r_codes[:, g, cols].bitcast(FP8X4),
+                scales=r_scales[:, g, cols],
+                in_=r_grouped[:].rearrange("p c t -> p (c t)"),
+            )
+
+        def second_layer(c):
+            for j in range(c * J_TILE, (c + 1) * J_TILE):
+                nodes = slice(j * NODES, (j + 1) * NODES)
+                for f in range(HALVES):
+                    feats = slice(f * BANK, (f + 1) * BANK)
+                    out_bank = psum.tile([P, BANK], F32, name="out_bank", tag="out_bank", bufs=2)
+                    for g in range(PASSES):
+                        nc.tensor.matmul_mx(
+                            out=out_bank[:],
+                            lhsT=r_codes[:, g, nodes].bitcast(FP8X4),
+                            lhsT_scale=r_scales[:, g, nodes],
+                            rhs=w_codes[:, M2_CHUNK + g, feats].bitcast(FP8X4),
+                            rhs_scale=w_scales[:, M2_CHUNK + g, feats],
+                            start=(g == 0),
+                            stop=(g == PASSES - 1),
+                        )
+                    nc.vector.scalar_tensor_tensor(
+                        out=acc[:, feats],
+                        in0=out_bank[:],
+                        scalar=mask[:, j : j + 1],
+                        in1=acc[:, feats],
+                        op0=MULT,
+                        op1=ADD,
+                    )
+
+        steps = [(c, g) for c in range(COL_TILES) for g in range(PASSES)]
+        next_pairs = pair_terms(0, 0)
+        for chunk in range(E2_CHUNK, E2_CHUNK + PASSES):
+            quantise_weights(chunk, W1_VECTOR_COLS)
+        quantise_edges(0)
+        for chunk in range(M2_CHUNK, M2_CHUNK + PASSES):
+            quantise_weights(chunk, 0)
+        for number, (c, g) in enumerate(steps):
+            pairs = next_pairs
+            if number + 1 < len(steps):
+                next_pairs = pair_terms(steps[number + 1][0], steps[number + 1][1])
+            if g == 0 and c + 1 < COL_TILES:
+                quantise_edges(c + 1)
+            first_layer(c, g, pairs)
+            if g == 0 and c > 0:
+                second_layer(c - 1)
+        second_layer(COL_TILES - 1)
+
+        for f in range(HALVES):
+            feats = slice(f * BANK, (f + 1) * BANK)
+            nc.sync.dma_start(out=out_rows[:, feats], in_=acc[:, feats])

@@ -30,7 +30,10 @@ RUN = 4
 
 XI_CHUNK, XJ_CHUNK, E2_CHUNK, M2_CHUNK = 0, 2, 4, 6
 WEIGHT_CHUNKS = 8
-W1_VECTOR_COLS = WIDTH // 2
+W1_VECTOR_COLS = BANK // 2
+PAIR_TILES = 8
+LATE_VECTOR_COLS = BANK // 4
+NODE_WEIGHTS_ROUND, EDGE_WEIGHTS_ROUND, M2_ROUND = 1, 2, 2
 
 FLOPS = 2 * WIDTH * WIDTH * (2 * NODES + 2 * EDGES)
 
@@ -44,12 +47,14 @@ def tile_messagepassing_pa_kernel(tc, h, e, adj_mask, W_m1, b_m1, W_m2, b_m2, ou
 
     with ExitStack() as stack:
         keep = stack.enter_context(tc.tile_pool(name="keep", bufs=1))
-        raw_pool = stack.enter_context(tc.tile_pool(name="raw", bufs=4))
+        raw_pool = stack.enter_context(tc.tile_pool(name="raw", bufs=6))
         edge_pool = stack.enter_context(tc.tile_pool(name="edge", bufs=3))
-        grouped_pool = stack.enter_context(tc.tile_pool(name="grouped", bufs=2))
+        grouped_pool = stack.enter_context(tc.tile_pool(name="grouped", bufs=8))
         stage = stack.enter_context(tc.tile_pool(name="stage", bufs=2))
-        pair_pool = stack.enter_context(tc.tile_pool(name="pair", bufs=2 * PACK))
-        psum = stack.enter_context(tc.psum_pool(name="psum", bufs=2))
+        pair_pool = stack.enter_context(tc.tile_pool(name="pair", bufs=PAIR_TILES))
+        psum = stack.enter_context(tc.psum_pool(name="psum", bufs=8))
+
+        stack.enter_context(tc.manual_schedule())
 
         b1_rows = keep.tile([P, P], BF16)
         nc.vector.memset(b1_rows[:], 0.0)
@@ -63,18 +68,17 @@ def tile_messagepassing_pa_kernel(tc, h, e, adj_mask, W_m1, b_m1, W_m2, b_m2, ou
         h_sb = keep.tile([P, WIDTH], BF16)
         nc.sync.dma_start(out=h_sb[:], in_=h_rows)
 
-        def load_w1_chunk(chunk):
-            raw = raw_pool.tile([P, PACK, WIDTH], BF16, name="raw", tag="raw")
-            rows = W_m1[chunk * K_PASS : (chunk + 1) * K_PASS, :]
-            nc.sync.dma_start(
-                out=raw[:].rearrange("p (u s) n -> p u s n", u=2),
-                in_=rows.rearrange("(u p s) n -> p u s n", u=2, s=2),
-            )
+        def load_w1_piece(chunk, half):
+            raw = raw_pool.tile([P, PACK, BANK], BF16, name="raw", tag="raw")
+            for u in range(2):
+                first = chunk * K_PASS + 2 * P * u
+                rows = W_m1[first : first + 2 * P, half * BANK : (half + 1) * BANK]
+                nc.sync.dma_start(out=raw[:, 2 * u : 2 * u + 2, :], in_=rows.rearrange("(p s) n -> p s n", s=2))
             return raw
 
-        def load_w2_chunk(g):
-            raw = raw_pool.tile([P, PACK, WIDTH], BF16, name="raw", tag="raw")
-            rows = W_m2[g * K_PASS : (g + 1) * K_PASS, :]
+        def load_w2_piece(g, half):
+            raw = raw_pool.tile([P, PACK, BANK], BF16, name="raw", tag="raw")
+            rows = W_m2[g * K_PASS : (g + 1) * K_PASS, half * BANK : (half + 1) * BANK]
             nc.sync.dma_start(out=raw[:], in_=rows.rearrange("(t p) n -> p t n", t=PACK))
             return raw
 
@@ -83,10 +87,21 @@ def tile_messagepassing_pa_kernel(tc, h, e, adj_mask, W_m1, b_m1, W_m2, b_m2, ou
             nc.sync.dma_start(out=e_sb[:], in_=e_rows[:, c * J_TILE : (c + 1) * J_TILE, :])
             return e_sb
 
-        raw_chunks = [load_w1_chunk(chunk) for chunk in range(M2_CHUNK)]
+        raw_pieces = {}
+        for chunk in range(XI_CHUNK, E2_CHUNK):
+            raw_pieces[(chunk, 0)] = load_w1_piece(chunk, 0)
         e_tiles = [load_edges(0)]
-        raw_chunks.extend([load_w2_chunk(g) for g in range(PASSES)])
-        e_tiles.extend([load_edges(c) for c in range(1, COL_TILES)])
+        for chunk in range(E2_CHUNK, M2_CHUNK):
+            raw_pieces[(chunk, 0)] = load_w1_piece(chunk, 0)
+        e_tiles.extend([load_edges(c) for c in range(1, COL_TILES - 1)])
+        for chunk in range(XI_CHUNK, E2_CHUNK):
+            raw_pieces[(chunk, 1)] = load_w1_piece(chunk, 1)
+        e_tiles.append(load_edges(COL_TILES - 1))
+        for chunk in range(E2_CHUNK, M2_CHUNK):
+            raw_pieces[(chunk, 1)] = load_w1_piece(chunk, 1)
+        for g in range(PASSES):
+            for half in range(HALVES):
+                raw_pieces[(M2_CHUNK + g, half)] = load_w2_piece(g, half)
 
         ident_f32 = keep.tile([P, P], F32)
         make_identity(nc, ident_f32[:])
@@ -110,58 +125,37 @@ def tile_messagepassing_pa_kernel(tc, h, e, adj_mask, W_m1, b_m1, W_m2, b_m2, ou
                 in_=raw[:, :, cols].rearrange("p t (c i) -> p c t i", i=RUN),
             )
 
-        def quantise_weights(chunk, vector_cols):
-            raw = raw_chunks[chunk]
-            grouped = grouped_pool.tile([P, WIDTH, PACK], BF16, name="grouped", tag="grouped", align_bytes=64)
+        grouped_pieces = {}
+
+        def regroup_weights(chunk, half, vector_cols):
+            raw = raw_pieces[(chunk, half)]
+            grouped = grouped_pool.tile([P, BANK, PACK], BF16, name="grouped", tag="grouped", align_bytes=64)
             if vector_cols > 0:
                 regroup(nc.vector.tensor_copy, grouped, raw, slice(0, vector_cols))
-            regroup(nc.scalar.copy, grouped, raw, slice(vector_cols, WIDTH))
+            if vector_cols < BANK:
+                regroup(nc.scalar.copy, grouped, raw, slice(vector_cols, BANK))
+            grouped_pieces[(chunk, half)] = grouped
+
+        def quantise_weights(chunk, half):
+            cols = slice(half * BANK, (half + 1) * BANK)
             nc.vector.quantize_mx(
-                out=w_codes[:, chunk, :].bitcast(FP8X4),
-                scales=w_scales[:, chunk, :],
-                in_=grouped[:].rearrange("p n t -> p (n t)"),
+                out=w_codes[:, chunk, cols].bitcast(FP8X4),
+                scales=w_scales[:, chunk, cols],
+                in_=grouped_pieces[(chunk, half)][:].rearrange("p n t -> p (n t)"),
             )
 
         def transpose_words(bank_cols, rows_bf16, g, u):
             first = (K_PASS * g + 2 * P * u) // 2
             nc.tensor.transpose(bank_cols, rows_bf16.bitcast(F32)[:, first : first + P], ident_f32[:])
 
-        h_bank = psum.tile([P, PASSES, 2, NODES], F32, name="h_bank", tag="small")
-        for g in range(PASSES):
-            for u in range(2):
-                transpose_words(h_bank[:, g, u, :], h_sb[:], g, u)
-        h_grouped = keep.tile([P, PASSES * NODES * PACK], BF16, align_bytes=64)
-        nc.vector.tensor_copy(
-            out=h_grouped[:].bitcast(F32).rearrange("p (g n u) -> p g n u", g=PASSES, u=2),
-            in_=h_bank[:].rearrange("p g u n -> p g n u"),
-        )
-        nc.vector.quantize_mx(
-            out=h_codes[:].rearrange("p g n -> p (g n)").bitcast(FP8X4),
-            scales=h_scales[:].rearrange("p g n -> p (g n)"),
-            in_=h_grouped[:],
-        )
-
-        b1_bank = psum.tile([P, P], BF16, name="b1_bank", tag="small")
-        nc.tensor.transpose(b1_bank[:], b1_rows[:], ident_bf16[:])
+        target_term = keep.tile([P, BLOCKS, NODES], F32)
+        source_term = keep.tile([P, BLOCKS, NODES], F32)
         b1 = keep.tile([P, BLOCKS], F32)
-        nc.vector.tensor_copy(out=b1[:], in_=b1_bank[:, 0:BLOCKS])
 
-        mask = keep.tile([P, GRAPH_NODES], F32)
-        nc.vector.tensor_copy(out=mask[:], in_=mask_bf16[:])
-        mask_sum = keep.tile([P, 1], F32)
-        nc.vector.tensor_reduce(out=mask_sum[:], in_=mask[:], axis=mybir.AxisListType.X, op=ADD)
+        node_banks = {}
 
-        acc = keep.tile([P, WIDTH], F32)
-        for f in range(HALVES):
-            feats = slice(f * BANK, (f + 1) * BANK)
-            b2_bank = psum.tile([P, BANK], F32, name="b2_bank", tag="small")
-            nc.tensor.matmul(out=b2_bank[:], lhsT=ones[:], rhs=b2_row[:, feats], start=True, stop=True)
-            nc.vector.scalar_tensor_tensor(
-                out=acc[:, feats], in0=b2_bank[:], scalar=mask_sum[:, 0:1], in1=h_sb[:, feats], op0=MULT, op1=ADD
-            )
-
-        def node_term_bank(first_chunk, half):
-            bank = psum.tile([P, PACK, NODES], F32, name="node_bank", tag="small")
+        def node_term_products(first_chunk, half):
+            bank = psum.tile([P, PACK, NODES], F32, name="node_bank", tag="bank")
             for t in range(PACK):
                 units = slice((PACK * half + t) * P, (PACK * half + t + 1) * P)
                 for kp in range(PASSES):
@@ -174,30 +168,32 @@ def tile_messagepassing_pa_kernel(tc, h, e, adj_mask, W_m1, b_m1, W_m2, b_m2, ou
                         start=(kp == 0),
                         stop=(kp == PASSES - 1),
                     )
-            return bank
+            node_banks[(first_chunk, half)] = bank
 
-        target_term = keep.tile([P, BLOCKS, NODES], F32)
-        source_term = keep.tile([P, BLOCKS, NODES], F32)
-
-        for chunk in range(XI_CHUNK, XI_CHUNK + PASSES):
-            quantise_weights(chunk, W1_VECTOR_COLS)
-        for half in range(BLOCKS // PACK):
+        def keep_node_terms(half):
             blocks = slice(PACK * half, PACK * (half + 1))
-            bank = node_term_bank(XI_CHUNK, half)
             nc.vector.tensor_tensor(
                 out=target_term[:, blocks, :],
-                in0=bank[:],
+                in0=node_banks[(XI_CHUNK, half)][:],
                 in1=b1[:, blocks].unsqueeze(2).to_broadcast([P, PACK, NODES]),
                 op=ADD,
             )
-        for chunk in range(XJ_CHUNK, XJ_CHUNK + PASSES):
-            quantise_weights(chunk, W1_VECTOR_COLS)
-        for half in range(BLOCKS // PACK):
-            blocks = slice(PACK * half, PACK * (half + 1))
-            bank = node_term_bank(XJ_CHUNK, half)
-            nc.scalar.copy(out=source_term[:, blocks, :], in_=bank[:])
+            nc.vector.tensor_copy(out=source_term[:, blocks, :], in_=node_banks[(XJ_CHUNK, half)][:])
 
-        def pair_terms(c, g):
+        def quantise_w1_pieces(half, first_chunk, last_chunk, vector_cols):
+            for chunk in range(first_chunk, last_chunk + 1):
+                if chunk < last_chunk:
+                    regroup_weights(chunk, half, vector_cols)
+                if chunk > first_chunk:
+                    quantise_weights(chunk - 1, half)
+                    if chunk == XI_CHUNK + PASSES:
+                        node_term_products(XI_CHUNK, half)
+                    if chunk == XJ_CHUNK + PASSES:
+                        node_term_products(XJ_CHUNK, half)
+
+        pairs = {}
+
+        def pair_terms(g, c):
             tiles = []
             for t in range(PACK):
                 block = PACK * g + t
@@ -215,33 +211,43 @@ def tile_messagepassing_pa_kernel(tc, h, e, adj_mask, W_m1, b_m1, W_m2, b_m2, ou
                     op=ADD,
                 )
                 tiles.append(pair)
-            return tiles
+            pairs[(g, c)] = tiles
 
-        def quantise_edges(c):
-            e_sb = e_tiles[c]
-            cols = slice(c * BANK, (c + 1) * BANK)
+        e_grouped_tiles = {}
+
+        def transpose_edges(c):
             for g in range(PASSES):
-                e_grouped = stage.tile([P, BANK * PACK], BF16, name="e_grouped", tag="e_grouped", align_bytes=64)
+                e_grouped = stage.tile([P, BANK * PACK], BF16, name="e_grouped", tag="e_grouped", bufs=4, align_bytes=64)
                 e_words = e_grouped[:].bitcast(F32).rearrange("p (x n u) -> p x n u", x=J_TILE, u=2)
                 for first_j in range(0, J_TILE, 2):
-                    e_bank = psum.tile([P, 2, 2, NODES], F32, name="e_bank", tag="small")
+                    e_bank = psum.tile([P, 2, 2, NODES], F32, name="e_bank", tag="bank")
                     for x in range(2):
                         for u in range(2):
-                            transpose_words(e_bank[:, x, u, :], e_sb[:, first_j + x, :], g, u)
+                            transpose_words(e_bank[:, x, u, :], e_tiles[c][:, first_j + x, :], g, u)
                     nc.scalar.copy(
                         out=e_words[:, first_j : first_j + 2, :, :],
                         in_=e_bank[:].rearrange("p x u n -> p x n u"),
                     )
+                e_grouped_tiles[(c, g)] = e_grouped
+
+        def quantise_edges(c):
+            cols = slice(c * BANK, (c + 1) * BANK)
+            for g in range(PASSES):
                 nc.vector.quantize_mx(
-                    out=e_codes[:, g, cols].bitcast(FP8X4), scales=e_scales[:, g, cols], in_=e_grouped[:]
+                    out=e_codes[:, g, cols].bitcast(FP8X4),
+                    scales=e_scales[:, g, cols],
+                    in_=e_grouped_tiles[(c, g)][:],
                 )
 
-        def first_layer(c, g, pairs):
+        edge_banks = {}
+        p_tiles = {}
+        r_grouped_tiles = {}
+
+        def first_layer_products(g, c):
             cols = slice(c * BANK, (c + 1) * BANK)
-            p_bf16 = stage.tile([P, PACK, BANK], BF16, name="p_bf16", tag="p_bf16")
             for t in range(PACK):
                 units = slice((PACK * g + t) * P, (PACK * g + t + 1) * P)
-                edge_bank = psum.tile([P, BANK], F32, name="edge_bank", tag="edge_bank", bufs=4)
+                edge_bank = psum.tile([P, BANK], F32, name="edge_bank", tag="bank")
                 for kp in range(PASSES):
                     nc.tensor.matmul_mx(
                         out=edge_bank[:],
@@ -252,30 +258,65 @@ def tile_messagepassing_pa_kernel(tc, h, e, adj_mask, W_m1, b_m1, W_m2, b_m2, ou
                         start=(kp == 0),
                         stop=(kp == PASSES - 1),
                     )
+                edge_banks[(g, c, t)] = edge_bank
+
+        def first_layer_sums(g, c):
+            p_bf16 = stage.tile([P, PACK, BANK], BF16, name="p_bf16", tag="p_bf16")
+            for t in range(PACK):
                 nc.vector.tensor_tensor(
                     out=p_bf16[:, t, :],
-                    in0=edge_bank[:],
-                    in1=pairs[t][:].rearrange("p j b i -> p (j b i)"),
+                    in0=edge_banks[(g, c, t)][:],
+                    in1=pairs[(g, c)][t][:].rearrange("p j b i -> p (j b i)"),
                     op=ADD,
                 )
+            p_tiles[(g, c)] = p_bf16
+
+        def first_layer_relu(g, c):
             r_grouped = stage.tile([P, BANK, PACK], BF16, name="r_grouped", tag="r_grouped", align_bytes=64)
             nc.scalar.activation(
                 out=r_grouped[:].rearrange("p (c i) t -> p c t i", i=RUN),
-                in_=p_bf16[:].rearrange("p t (c i) -> p c t i", i=RUN),
+                in_=p_tiles[(g, c)][:].rearrange("p t (c i) -> p c t i", i=RUN),
                 func=RELU,
             )
+            r_grouped_tiles[(g, c)] = r_grouped
+
+        def quantise_hidden(g, c):
+            cols = slice(c * BANK, (c + 1) * BANK)
             nc.vector.quantize_mx(
                 out=r_codes[:, g, cols].bitcast(FP8X4),
                 scales=r_scales[:, g, cols],
-                in_=r_grouped[:].rearrange("p c t -> p (c t)"),
+                in_=r_grouped_tiles[(g, c)][:].rearrange("p c t -> p (c t)"),
             )
+
+        mask = keep.tile([P, GRAPH_NODES], F32)
+        mask_sum = keep.tile([P, 1], F32)
+        acc = keep.tile([P, WIDTH], F32)
+
+        b2_banks = []
+
+        def spread_b2():
+            for f in range(HALVES):
+                b2_bank = psum.tile([P, BANK], F32, name="b2_bank", tag="bank")
+                nc.tensor.matmul(
+                    out=b2_bank[:], lhsT=ones[:], rhs=b2_row[:, f * BANK : (f + 1) * BANK], start=True, stop=True
+                )
+                b2_banks.append(b2_bank)
+
+        def start_sum():
+            nc.vector.tensor_copy(out=mask[:], in_=mask_bf16[:])
+            nc.vector.tensor_reduce(out=mask_sum[:], in_=mask[:], axis=mybir.AxisListType.X, op=ADD)
+            for f in range(HALVES):
+                feats = slice(f * BANK, (f + 1) * BANK)
+                nc.vector.scalar_tensor_tensor(
+                    out=acc[:, feats], in0=b2_banks[f][:], scalar=mask_sum[:, 0:1], in1=h_sb[:, feats], op0=MULT, op1=ADD
+                )
 
         def second_layer(c):
             for j in range(c * J_TILE, (c + 1) * J_TILE):
                 nodes = slice(j * NODES, (j + 1) * NODES)
                 for f in range(HALVES):
                     feats = slice(f * BANK, (f + 1) * BANK)
-                    out_bank = psum.tile([P, BANK], F32, name="out_bank", tag="out_bank", bufs=2)
+                    out_bank = psum.tile([P, BANK], F32, name="out_bank", tag="bank")
                     for g in range(PASSES):
                         nc.tensor.matmul_mx(
                             out=out_bank[:],
@@ -295,23 +336,82 @@ def tile_messagepassing_pa_kernel(tc, h, e, adj_mask, W_m1, b_m1, W_m2, b_m2, ou
                         op1=ADD,
                     )
 
-        steps = [(c, g) for c in range(COL_TILES) for g in range(PASSES)]
-        next_pairs = pair_terms(0, 0)
-        for chunk in range(E2_CHUNK, E2_CHUNK + PASSES):
-            quantise_weights(chunk, W1_VECTOR_COLS)
+        h_bank = psum.tile([P, PASSES, 2, NODES], F32, name="h_bank", tag="bank")
+        for g in range(PASSES):
+            for u in range(2):
+                transpose_words(h_bank[:, g, u, :], h_sb[:], g, u)
+        h_grouped = keep.tile([P, PASSES * NODES * PACK], BF16, align_bytes=64)
+        nc.vector.tensor_copy(
+            out=h_grouped[:].bitcast(F32).rearrange("p (g n u) -> p g n u", g=PASSES, u=2),
+            in_=h_bank[:].rearrange("p g u n -> p g n u"),
+        )
+        b1_bank = psum.tile([P, P], BF16, name="b1_bank", tag="bank")
+        nc.tensor.transpose(b1_bank[:], b1_rows[:], ident_bf16[:])
+        nc.vector.tensor_copy(out=b1[:], in_=b1_bank[:, 0:BLOCKS])
+        nc.vector.quantize_mx(
+            out=h_codes[:].rearrange("p g n -> p (g n)").bitcast(FP8X4),
+            scales=h_scales[:].rearrange("p g n -> p (g n)"),
+            in_=h_grouped[:],
+        )
+
+        spread_b2()
+
+        quantise_w1_pieces(0, XI_CHUNK, E2_CHUNK, W1_VECTOR_COLS)
+        start_sum()
+        keep_node_terms(0)
+        for c in range(COL_TILES):
+            pair_terms(0, c)
+        transpose_edges(0)
+        quantise_w1_pieces(0, E2_CHUNK, M2_CHUNK, BANK)
         quantise_edges(0)
-        for chunk in range(M2_CHUNK, M2_CHUNK + PASSES):
-            quantise_weights(chunk, 0)
-        for number, (c, g) in enumerate(steps):
-            pairs = next_pairs
-            if number + 1 < len(steps):
-                next_pairs = pair_terms(steps[number + 1][0], steps[number + 1][1])
-            if g == 0 and c + 1 < COL_TILES:
-                quantise_edges(c + 1)
-            first_layer(c, g, pairs)
-            if g == 0 and c > 0:
-                second_layer(c - 1)
-        second_layer(COL_TILES - 1)
+        transpose_edges(1)
+        first_layer_products(0, 0)
+
+        steps = [(g, c) for g in range(PASSES) for c in range(COL_TILES)]
+        node_pieces = [(chunk, 1) for chunk in range(XI_CHUNK, E2_CHUNK)]
+        edge_pieces = [(chunk, 1) for chunk in range(E2_CHUNK, M2_CHUNK)]
+        m2_pieces = [(M2_CHUNK + g, half) for g in range(PASSES) for half in range(HALVES)]
+
+        def regroup_in_round(n, round_of_pieces, pieces, vector_cols):
+            if n == round_of_pieces:
+                for chunk, half in pieces:
+                    regroup_weights(chunk, half, vector_cols)
+
+        def quantise_in_round(n, round_of_pieces, pieces):
+            if n == round_of_pieces + 1:
+                for chunk, half in pieces:
+                    quantise_weights(chunk, half)
+
+        for n in range(len(steps) + 2):
+            if 1 <= n <= len(steps):
+                first_layer_relu(steps[n - 1][0], steps[n - 1][1])
+            if n >= 2:
+                quantise_hidden(steps[n - 2][0], steps[n - 2][1])
+            regroup_in_round(n, NODE_WEIGHTS_ROUND, node_pieces, LATE_VECTOR_COLS)
+            regroup_in_round(n, EDGE_WEIGHTS_ROUND, edge_pieces, LATE_VECTOR_COLS)
+            for number, piece in enumerate(m2_pieces):
+                regroup_in_round(n, M2_ROUND + number, [piece], 0)
+            if n < len(steps):
+                first_layer_sums(steps[n][0], steps[n][1])
+            quantise_in_round(n, NODE_WEIGHTS_ROUND, node_pieces)
+            quantise_in_round(n, EDGE_WEIGHTS_ROUND, edge_pieces)
+            for number, piece in enumerate(m2_pieces):
+                quantise_in_round(n, M2_ROUND + number, [piece])
+            if n == NODE_WEIGHTS_ROUND + 1:
+                node_term_products(XI_CHUNK, 1)
+                node_term_products(XJ_CHUNK, 1)
+            if n >= 2 and steps[n - 2][0] == PASSES - 1:
+                second_layer(steps[n - 2][1])
+            if n + 2 < COL_TILES:
+                transpose_edges(n + 2)
+            if n + 1 < COL_TILES:
+                quantise_edges(n + 1)
+            if n == NODE_WEIGHTS_ROUND + 1:
+                keep_node_terms(1)
+                for c in range(COL_TILES):
+                    pair_terms(1, c)
+            if n + 1 < len(steps):
+                first_layer_products(steps[n + 1][0], steps[n + 1][1])
 
         for f in range(HALVES):
             feats = slice(f * BANK, (f + 1) * BANK)

@@ -31,7 +31,6 @@ RUN = 4
 XI_CHUNK, XJ_CHUNK, E2_CHUNK, M2_CHUNK = 0, 2, 4, 6
 WEIGHT_CHUNKS = 8
 W1_VECTOR_COLS = BANK // 2
-PAIR_TILES = 8
 LATE_VECTOR_COLS = BANK // 4
 NODE_WEIGHTS_ROUND, EDGE_WEIGHTS_ROUND, M2_ROUND = 1, 2, 2
 
@@ -51,7 +50,6 @@ def tile_messagepassing_pa_kernel(tc, h, e, adj_mask, W_m1, b_m1, W_m2, b_m2, ou
         edge_pool = stack.enter_context(tc.tile_pool(name="edge", bufs=3))
         grouped_pool = stack.enter_context(tc.tile_pool(name="grouped", bufs=8))
         stage = stack.enter_context(tc.tile_pool(name="stage", bufs=2))
-        pair_pool = stack.enter_context(tc.tile_pool(name="pair", bufs=PAIR_TILES))
         psum = stack.enter_context(tc.psum_pool(name="psum", bufs=8))
 
         stack.enter_context(tc.manual_schedule())
@@ -112,8 +110,8 @@ def tile_messagepassing_pa_kernel(tc, h, e, adj_mask, W_m1, b_m1, W_m2, b_m2, ou
 
         w_codes = keep.tile([P, WEIGHT_CHUNKS, WIDTH], U32, align_bytes=64)
         w_scales = keep.tile([P, WEIGHT_CHUNKS, WIDTH], U8, align_bytes=64)
-        h_codes = keep.tile([P, PASSES, NODES], U32, align_bytes=64)
-        h_scales = keep.tile([P, PASSES, NODES], U8, align_bytes=64)
+        h_codes = keep.tile([P, PASSES, BANK], U32, align_bytes=64)
+        h_scales = keep.tile([P, PASSES, BANK], U8, align_bytes=64)
         e_codes = keep.tile([P, PASSES, EDGES], U32, align_bytes=64)
         e_scales = keep.tile([P, PASSES, EDGES], U8, align_bytes=64)
         r_codes = keep.tile([P, PASSES, EDGES], U32, align_bytes=64)
@@ -148,37 +146,34 @@ def tile_messagepassing_pa_kernel(tc, h, e, adj_mask, W_m1, b_m1, W_m2, b_m2, ou
             first = (K_PASS * g + 2 * P * u) // 2
             nc.tensor.transpose(bank_cols, rows_bf16.bitcast(F32)[:, first : first + P], ident_f32[:])
 
-        target_term = keep.tile([P, BLOCKS, NODES], F32)
         source_term = keep.tile([P, BLOCKS, NODES], F32)
         b1 = keep.tile([P, BLOCKS], F32)
+        source_banks = {}
 
-        node_banks = {}
-
-        def node_term_products(first_chunk, half):
-            bank = psum.tile([P, PACK, NODES], F32, name="node_bank", tag="bank")
+        def source_term_products(half):
+            bank = psum.tile([P, PACK, NODES], F32, name="source_bank", tag="bank")
             for t in range(PACK):
                 units = slice((PACK * half + t) * P, (PACK * half + t + 1) * P)
                 for kp in range(PASSES):
                     nc.tensor.matmul_mx(
                         out=bank[:, t, :],
-                        lhsT=w_codes[:, first_chunk + kp, units].bitcast(FP8X4),
-                        lhsT_scale=w_scales[:, first_chunk + kp, units],
-                        rhs=h_codes[:, kp, :].bitcast(FP8X4),
-                        rhs_scale=h_scales[:, kp, :],
+                        lhsT=w_codes[:, XJ_CHUNK + kp, units].bitcast(FP8X4),
+                        lhsT_scale=w_scales[:, XJ_CHUNK + kp, units],
+                        rhs=h_codes[:, kp, 0:NODES].bitcast(FP8X4),
+                        rhs_scale=h_scales[:, kp, 0:NODES],
                         start=(kp == 0),
                         stop=(kp == PASSES - 1),
                     )
-            node_banks[(first_chunk, half)] = bank
+            source_banks[half] = bank
 
-        def keep_node_terms(half):
+        def keep_source_term(half):
             blocks = slice(PACK * half, PACK * (half + 1))
             nc.vector.tensor_tensor(
-                out=target_term[:, blocks, :],
-                in0=node_banks[(XI_CHUNK, half)][:],
+                out=source_term[:, blocks, :],
+                in0=source_banks[half][:],
                 in1=b1[:, blocks].unsqueeze(2).to_broadcast([P, PACK, NODES]),
                 op=ADD,
             )
-            nc.vector.tensor_copy(out=source_term[:, blocks, :], in_=node_banks[(XJ_CHUNK, half)][:])
 
         def quantise_w1_pieces(half, first_chunk, last_chunk, vector_cols):
             for chunk in range(first_chunk, last_chunk + 1):
@@ -186,32 +181,8 @@ def tile_messagepassing_pa_kernel(tc, h, e, adj_mask, W_m1, b_m1, W_m2, b_m2, ou
                     regroup_weights(chunk, half, vector_cols)
                 if chunk > first_chunk:
                     quantise_weights(chunk - 1, half)
-                    if chunk == XI_CHUNK + PASSES:
-                        node_term_products(XI_CHUNK, half)
                     if chunk == XJ_CHUNK + PASSES:
-                        node_term_products(XJ_CHUNK, half)
-
-        pairs = {}
-
-        def pair_terms(g, c):
-            tiles = []
-            for t in range(PACK):
-                block = PACK * g + t
-                pair = pair_pool.tile([P, J_TILE, GRAPHS, GRAPH_NODES], F32, name="pair", tag="pair")
-                nc.gpsimd.tensor_tensor(
-                    out=pair[:],
-                    in0=target_term[:, block, :]
-                    .rearrange("p (b i) -> p b i", b=GRAPHS)
-                    .unsqueeze(1)
-                    .to_broadcast([P, J_TILE, GRAPHS, GRAPH_NODES]),
-                    in1=source_term[:, block, :]
-                    .rearrange("p (b j) -> p j b", b=GRAPHS)[:, c * J_TILE : (c + 1) * J_TILE, :]
-                    .unsqueeze(3)
-                    .to_broadcast([P, J_TILE, GRAPHS, GRAPH_NODES]),
-                    op=ADD,
-                )
-                tiles.append(pair)
-            pairs[(g, c)] = tiles
+                        source_term_products(half)
 
         e_grouped_tiles = {}
 
@@ -243,30 +214,47 @@ def tile_messagepassing_pa_kernel(tc, h, e, adj_mask, W_m1, b_m1, W_m2, b_m2, ou
         p_tiles = {}
         r_grouped_tiles = {}
 
-        def first_layer_products(g, c):
-            cols = slice(c * BANK, (c + 1) * BANK)
+        def target_products(g, c):
             for t in range(PACK):
                 units = slice((PACK * g + t) * P, (PACK * g + t + 1) * P)
                 edge_bank = psum.tile([P, BANK], F32, name="edge_bank", tag="bank")
                 for kp in range(PASSES):
                     nc.tensor.matmul_mx(
                         out=edge_bank[:],
+                        lhsT=w_codes[:, XI_CHUNK + kp, units].bitcast(FP8X4),
+                        lhsT_scale=w_scales[:, XI_CHUNK + kp, units],
+                        rhs=h_codes[:, kp, :].bitcast(FP8X4),
+                        rhs_scale=h_scales[:, kp, :],
+                        start=(kp == 0),
+                        stop=False,
+                    )
+                edge_banks[(g, c, t)] = edge_bank
+
+        def edge_products(g, c):
+            cols = slice(c * BANK, (c + 1) * BANK)
+            for t in range(PACK):
+                units = slice((PACK * g + t) * P, (PACK * g + t + 1) * P)
+                for kp in range(PASSES):
+                    nc.tensor.matmul_mx(
+                        out=edge_banks[(g, c, t)][:],
                         lhsT=w_codes[:, E2_CHUNK + kp, units].bitcast(FP8X4),
                         lhsT_scale=w_scales[:, E2_CHUNK + kp, units],
                         rhs=e_codes[:, kp, cols].bitcast(FP8X4),
                         rhs_scale=e_scales[:, kp, cols],
-                        start=(kp == 0),
+                        start=False,
                         stop=(kp == PASSES - 1),
                     )
-                edge_banks[(g, c, t)] = edge_bank
 
         def first_layer_sums(g, c):
             p_bf16 = stage.tile([P, PACK, BANK], BF16, name="p_bf16", tag="p_bf16")
             for t in range(PACK):
                 nc.vector.tensor_tensor(
-                    out=p_bf16[:, t, :],
-                    in0=edge_banks[(g, c, t)][:],
-                    in1=pairs[(g, c)][t][:].rearrange("p j b i -> p (j b i)"),
+                    out=p_bf16[:, t, :].rearrange("p (j b i) -> p j b i", j=J_TILE, b=GRAPHS),
+                    in0=edge_banks[(g, c, t)][:].rearrange("p (j b i) -> p j b i", j=J_TILE, b=GRAPHS),
+                    in1=source_term[:, PACK * g + t, :]
+                    .rearrange("p (b j) -> p j b", b=GRAPHS)[:, c * J_TILE : (c + 1) * J_TILE, :]
+                    .unsqueeze(3)
+                    .to_broadcast([P, J_TILE, GRAPHS, GRAPH_NODES]),
                     op=ADD,
                 )
             p_tiles[(g, c)] = p_bf16
@@ -340,32 +328,31 @@ def tile_messagepassing_pa_kernel(tc, h, e, adj_mask, W_m1, b_m1, W_m2, b_m2, ou
         for g in range(PASSES):
             for u in range(2):
                 transpose_words(h_bank[:, g, u, :], h_sb[:], g, u)
-        h_grouped = keep.tile([P, PASSES * NODES * PACK], BF16, align_bytes=64)
-        nc.vector.tensor_copy(
-            out=h_grouped[:].bitcast(F32).rearrange("p (g n u) -> p g n u", g=PASSES, u=2),
-            in_=h_bank[:].rearrange("p g u n -> p g n u"),
-        )
+        h_grouped = keep.tile([P, PASSES, BANK * PACK], BF16, align_bytes=64)
+        for g in range(PASSES):
+            nc.vector.tensor_copy(
+                out=h_grouped[:, g, :].bitcast(F32).rearrange("p (x n u) -> p x n u", x=J_TILE, u=2),
+                in_=h_bank[:, g, :, :].rearrange("p u n -> p n u").unsqueeze(1).to_broadcast([P, J_TILE, NODES, 2]),
+            )
         b1_bank = psum.tile([P, P], BF16, name="b1_bank", tag="bank")
         nc.tensor.transpose(b1_bank[:], b1_rows[:], ident_bf16[:])
         nc.vector.tensor_copy(out=b1[:], in_=b1_bank[:, 0:BLOCKS])
-        nc.vector.quantize_mx(
-            out=h_codes[:].rearrange("p g n -> p (g n)").bitcast(FP8X4),
-            scales=h_scales[:].rearrange("p g n -> p (g n)"),
-            in_=h_grouped[:],
-        )
+        for g in range(PASSES):
+            nc.vector.quantize_mx(
+                out=h_codes[:, g, :].bitcast(FP8X4), scales=h_scales[:, g, :], in_=h_grouped[:, g, :]
+            )
 
         spread_b2()
 
         quantise_w1_pieces(0, XI_CHUNK, E2_CHUNK, W1_VECTOR_COLS)
         start_sum()
-        keep_node_terms(0)
-        for c in range(COL_TILES):
-            pair_terms(0, c)
+        keep_source_term(0)
         transpose_edges(0)
         quantise_w1_pieces(0, E2_CHUNK, M2_CHUNK, BANK)
+        target_products(0, 0)
         quantise_edges(0)
         transpose_edges(1)
-        first_layer_products(0, 0)
+        edge_products(0, 0)
 
         steps = [(g, c) for g in range(PASSES) for c in range(COL_TILES)]
         node_pieces = [(chunk, 1) for chunk in range(XI_CHUNK, E2_CHUNK)]
@@ -398,20 +385,19 @@ def tile_messagepassing_pa_kernel(tc, h, e, adj_mask, W_m1, b_m1, W_m2, b_m2, ou
             for number, piece in enumerate(m2_pieces):
                 quantise_in_round(n, M2_ROUND + number, [piece])
             if n == NODE_WEIGHTS_ROUND + 1:
-                node_term_products(XI_CHUNK, 1)
-                node_term_products(XJ_CHUNK, 1)
+                source_term_products(1)
             if n >= 2 and steps[n - 2][0] == PASSES - 1:
                 second_layer(steps[n - 2][1])
             if n + 2 < COL_TILES:
                 transpose_edges(n + 2)
+            if n + 1 < len(steps):
+                target_products(steps[n + 1][0], steps[n + 1][1])
             if n + 1 < COL_TILES:
                 quantise_edges(n + 1)
             if n == NODE_WEIGHTS_ROUND + 1:
-                keep_node_terms(1)
-                for c in range(COL_TILES):
-                    pair_terms(1, c)
+                keep_source_term(1)
             if n + 1 < len(steps):
-                first_layer_products(steps[n + 1][0], steps[n + 1][1])
+                edge_products(steps[n + 1][0], steps[n + 1][1])
 
         for f in range(HALVES):
             feats = slice(f * BANK, (f + 1) * BANK)

@@ -52,7 +52,6 @@ def tile_messagepassing_pa_kernel(tc, h, e, adj_mask, W_m1, b_m1, W_m2, b_m2, ou
         stage = stack.enter_context(tc.tile_pool(name="stage", bufs=2))
         psum = stack.enter_context(tc.psum_pool(name="psum", bufs=8))
 
-        stack.enter_context(tc.manual_schedule())
 
         b1_rows = keep.tile([P, P], BF16)
         nc.vector.memset(b1_rows[:], 0.0)

@@ -11,6 +11,8 @@ U8 = mybir.dt.uint8
 ADD = mybir.AluOpType.add
 MULT = mybir.AluOpType.mult
 RELU = mybir.ActivationFunctionType.Relu
+IDENTITY = mybir.ActivationFunctionType.Identity
+COPY = mybir.ActivationFunctionType.Copy
 
 P = 128
 PACK = 4
@@ -31,8 +33,8 @@ RUN = 4
 XI_CHUNK, XJ_CHUNK, E2_CHUNK, M2_CHUNK = 0, 2, 4, 6
 WEIGHT_CHUNKS = 8
 W1_VECTOR_COLS = BANK // 2
-LATE_VECTOR_COLS = BANK // 4
-NODE_WEIGHTS_ROUND, EDGE_WEIGHTS_ROUND, M2_ROUND = 1, 2, 2
+LATE_VECTOR_COLS = 3 * BANK // 4
+RELU_DELAY, QUANT_DELAY = 2, 3
 
 FLOPS = 2 * WIDTH * WIDTH * (2 * NODES + 2 * EDGES)
 
@@ -48,9 +50,13 @@ def tile_messagepassing_pa_kernel(tc, h, e, adj_mask, W_m1, b_m1, W_m2, b_m2, ou
         keep = stack.enter_context(tc.tile_pool(name="keep", bufs=1))
         raw_pool = stack.enter_context(tc.tile_pool(name="raw", bufs=6))
         edge_pool = stack.enter_context(tc.tile_pool(name="edge", bufs=3))
-        grouped_pool = stack.enter_context(tc.tile_pool(name="grouped", bufs=8))
-        stage = stack.enter_context(tc.tile_pool(name="stage", bufs=2))
-        psum = stack.enter_context(tc.psum_pool(name="psum", bufs=8))
+        grouped_pool = stack.enter_context(tc.tile_pool(name="grouped", bufs=6))
+        stage = stack.enter_context(tc.tile_pool(name="stage", bufs=3))
+        psum = stack.enter_context(tc.psum_pool(name="psum", bufs=5))
+        psum_short = stack.enter_context(tc.psum_pool(name="psum_short", bufs=3))
+        stack.enter_context(
+            tc.manual_schedule(engines={mybir.EngineType.PE, mybir.EngineType.Activation, mybir.EngineType.DVE})
+        )
 
 
         b1_rows = keep.tile([P, P], BF16)
@@ -85,20 +91,22 @@ def tile_messagepassing_pa_kernel(tc, h, e, adj_mask, W_m1, b_m1, W_m2, b_m2, ou
             return e_sb
 
         raw_pieces = {}
-        for chunk in range(XI_CHUNK, E2_CHUNK):
+        for chunk in range(XI_CHUNK, XJ_CHUNK):
             raw_pieces[(chunk, 0)] = load_w1_piece(chunk, 0)
         e_tiles = [load_edges(0)]
-        for chunk in range(E2_CHUNK, M2_CHUNK):
+        for chunk in range(XJ_CHUNK, M2_CHUNK):
             raw_pieces[(chunk, 0)] = load_w1_piece(chunk, 0)
         e_tiles.extend([load_edges(c) for c in range(1, COL_TILES - 1)])
-        for chunk in range(XI_CHUNK, E2_CHUNK):
+        for chunk in range(XI_CHUNK, M2_CHUNK):
             raw_pieces[(chunk, 1)] = load_w1_piece(chunk, 1)
         e_tiles.append(load_edges(COL_TILES - 1))
-        for chunk in range(E2_CHUNK, M2_CHUNK):
-            raw_pieces[(chunk, 1)] = load_w1_piece(chunk, 1)
-        for g in range(PASSES):
-            for half in range(HALVES):
+        for half in range(HALVES):
+            for g in range(PASSES):
                 raw_pieces[(M2_CHUNK + g, half)] = load_w2_piece(g, half)
+
+        warm = keep.tile([P, 1], F32)
+        nc.vector.memset(warm[:], 0.0)
+        nc.scalar.activation(out=warm[:], in_=warm[:], func=RELU)
 
         ident_f32 = keep.tile([P, P], F32)
         make_identity(nc, ident_f32[:])
@@ -150,7 +158,7 @@ def tile_messagepassing_pa_kernel(tc, h, e, adj_mask, W_m1, b_m1, W_m2, b_m2, ou
         source_banks = {}
 
         def source_term_products(half):
-            bank = psum.tile([P, PACK, NODES], F32, name="source_bank", tag="bank")
+            bank = psum_short.tile([P, PACK, NODES], F32, name="source_bank", tag="short")
             for t in range(PACK):
                 units = slice((PACK * half + t) * P, (PACK * half + t + 1) * P)
                 for kp in range(PASSES):
@@ -166,55 +174,45 @@ def tile_messagepassing_pa_kernel(tc, h, e, adj_mask, W_m1, b_m1, W_m2, b_m2, ou
             source_banks[half] = bank
 
         def keep_source_term(half):
-            blocks = slice(PACK * half, PACK * (half + 1))
-            nc.vector.tensor_tensor(
-                out=source_term[:, blocks, :],
-                in0=source_banks[half][:],
-                in1=b1[:, blocks].unsqueeze(2).to_broadcast([P, PACK, NODES]),
-                op=ADD,
-            )
-
-        def quantise_w1_pieces(half, first_chunk, last_chunk, vector_cols):
-            for chunk in range(first_chunk, last_chunk + 1):
-                if chunk < last_chunk:
-                    regroup_weights(chunk, half, vector_cols)
-                if chunk > first_chunk:
-                    quantise_weights(chunk - 1, half)
-                    if chunk == XJ_CHUNK + PASSES:
-                        source_term_products(half)
+            for t in range(PACK):
+                block = PACK * half + t
+                nc.scalar.activation(
+                    out=source_term[:, block, :], in_=source_banks[half][:, t, :], func=IDENTITY, bias=b1[:, block : block + 1]
+                )
 
         e_grouped_tiles = {}
 
-        def transpose_edges(c):
-            for g in range(PASSES):
-                e_grouped = stage.tile([P, BANK * PACK], BF16, name="e_grouped", tag="e_grouped", bufs=4, align_bytes=64)
-                e_words = e_grouped[:].bitcast(F32).rearrange("p (x n u) -> p x n u", x=J_TILE, u=2)
-                for first_j in range(0, J_TILE, 2):
-                    e_bank = psum.tile([P, 2, 2, NODES], F32, name="e_bank", tag="bank")
-                    for x in range(2):
-                        for u in range(2):
-                            transpose_words(e_bank[:, x, u, :], e_tiles[c][:, first_j + x, :], g, u)
-                    nc.scalar.copy(
-                        out=e_words[:, first_j : first_j + 2, :, :],
-                        in_=e_bank[:].rearrange("p x u n -> p x n u"),
+        def transpose_edges(c, banks):
+            for number in banks:
+                g, first_j = number // 2, 2 * (number % 2)
+                if first_j == 0:
+                    e_grouped_tiles[(c, g)] = stage.tile(
+                        [P, BANK * PACK], BF16, name="e_grouped", tag="e_grouped", bufs=4, align_bytes=64
                     )
-                e_grouped_tiles[(c, g)] = e_grouped
-
-        def quantise_edges(c):
-            cols = slice(c * BANK, (c + 1) * BANK)
-            for g in range(PASSES):
-                nc.vector.quantize_mx(
-                    out=e_codes[:, g, cols].bitcast(FP8X4),
-                    scales=e_scales[:, g, cols],
-                    in_=e_grouped_tiles[(c, g)][:],
+                e_words = e_grouped_tiles[(c, g)][:].bitcast(F32).rearrange("p (x n u) -> p x n u", x=J_TILE, u=2)
+                e_bank = psum_short.tile([P, 2, 2, NODES], F32, name="e_bank", tag="short")
+                for x in range(2):
+                    for u in range(2):
+                        transpose_words(e_bank[:, x, u, :], e_tiles[c][:, first_j + x, :], g, u)
+                nc.scalar.copy(
+                    out=e_words[:, first_j : first_j + 2, :, :],
+                    in_=e_bank[:].rearrange("p x u n -> p x n u"),
                 )
+
+        def quantise_edges(c, g):
+            cols = slice(c * BANK, (c + 1) * BANK)
+            nc.vector.quantize_mx(
+                out=e_codes[:, g, cols].bitcast(FP8X4),
+                scales=e_scales[:, g, cols],
+                in_=e_grouped_tiles[(c, g)][:],
+            )
 
         edge_banks = {}
         p_tiles = {}
         r_grouped_tiles = {}
 
-        def target_products(g, c):
-            for t in range(PACK):
+        def target_products(g, c, blocks):
+            for t in blocks:
                 units = slice((PACK * g + t) * P, (PACK * g + t + 1) * P)
                 edge_bank = psum.tile([P, BANK], F32, name="edge_bank", tag="bank")
                 for kp in range(PASSES):
@@ -229,9 +227,9 @@ def tile_messagepassing_pa_kernel(tc, h, e, adj_mask, W_m1, b_m1, W_m2, b_m2, ou
                     )
                 edge_banks[(g, c, t)] = edge_bank
 
-        def edge_products(g, c):
+        def edge_products(g, c, blocks):
             cols = slice(c * BANK, (c + 1) * BANK)
-            for t in range(PACK):
+            for t in blocks:
                 units = slice((PACK * g + t) * P, (PACK * g + t + 1) * P)
                 for kp in range(PASSES):
                     nc.tensor.matmul_mx(
@@ -244,19 +242,18 @@ def tile_messagepassing_pa_kernel(tc, h, e, adj_mask, W_m1, b_m1, W_m2, b_m2, ou
                         stop=(kp == PASSES - 1),
                     )
 
-        def first_layer_sums(g, c):
-            p_bf16 = stage.tile([P, PACK, BANK], BF16, name="p_bf16", tag="p_bf16")
-            for t in range(PACK):
-                nc.vector.tensor_tensor(
-                    out=p_bf16[:, t, :].rearrange("p (j b i) -> p j b i", j=J_TILE, b=GRAPHS),
-                    in0=edge_banks[(g, c, t)][:].rearrange("p (j b i) -> p j b i", j=J_TILE, b=GRAPHS),
-                    in1=source_term[:, PACK * g + t, :]
-                    .rearrange("p (b j) -> p j b", b=GRAPHS)[:, c * J_TILE : (c + 1) * J_TILE, :]
-                    .unsqueeze(3)
-                    .to_broadcast([P, J_TILE, GRAPHS, GRAPH_NODES]),
-                    op=ADD,
-                )
-            p_tiles[(g, c)] = p_bf16
+        def first_layer_sum(g, c, t):
+            if t == 0:
+                p_tiles[(g, c)] = stage.tile([P, PACK, BANK], BF16, name="p_bf16", tag="p_bf16", bufs=4)
+            nc.vector.tensor_tensor(
+                out=p_tiles[(g, c)][:, t, :].rearrange("p (j b i) -> p j b i", j=J_TILE, b=GRAPHS),
+                in0=edge_banks[(g, c, t)][:].rearrange("p (j b i) -> p j b i", j=J_TILE, b=GRAPHS),
+                in1=source_term[:, PACK * g + t, :]
+                .rearrange("p (b j) -> p j b", b=GRAPHS)[:, c * J_TILE : (c + 1) * J_TILE, :]
+                .unsqueeze(3)
+                .to_broadcast([P, J_TILE, GRAPHS, GRAPH_NODES]),
+                op=ADD,
+            )
 
         def first_layer_relu(g, c):
             r_grouped = stage.tile([P, BANK, PACK], BF16, name="r_grouped", tag="r_grouped", align_bytes=64)
@@ -278,125 +275,154 @@ def tile_messagepassing_pa_kernel(tc, h, e, adj_mask, W_m1, b_m1, W_m2, b_m2, ou
         mask = keep.tile([P, GRAPH_NODES], F32)
         mask_sum = keep.tile([P, 1], F32)
         acc = keep.tile([P, WIDTH], F32)
-
-        b2_banks = []
-
-        def spread_b2():
-            for f in range(HALVES):
-                b2_bank = psum.tile([P, BANK], F32, name="b2_bank", tag="bank")
-                nc.tensor.matmul(
-                    out=b2_bank[:], lhsT=ones[:], rhs=b2_row[:, f * BANK : (f + 1) * BANK], start=True, stop=True
-                )
-                b2_banks.append(b2_bank)
+        b2_term = keep.tile([P, WIDTH], F32)
+        nc.vector.tensor_copy(out=mask[:], in_=mask_bf16[:])
+        nc.vector.tensor_reduce(out=mask_sum[:], in_=mask[:], axis=mybir.AxisListType.X, op=ADD)
 
         def start_sum():
-            nc.vector.tensor_copy(out=mask[:], in_=mask_bf16[:])
-            nc.vector.tensor_reduce(out=mask_sum[:], in_=mask[:], axis=mybir.AxisListType.X, op=ADD)
             for f in range(HALVES):
                 feats = slice(f * BANK, (f + 1) * BANK)
-                nc.vector.scalar_tensor_tensor(
-                    out=acc[:, feats], in0=b2_banks[f][:], scalar=mask_sum[:, 0:1], in1=h_sb[:, feats], op0=MULT, op1=ADD
+                b2_bank = psum_short.tile([P, BANK], F32, name="b2_bank", tag="short")
+                nc.tensor.matmul(out=b2_bank[:], lhsT=ones[:], rhs=b2_row[:, feats], start=True, stop=True)
+                nc.scalar.activation(out=b2_term[:, feats], in_=b2_bank[:], func=COPY, scale=mask_sum[:, 0:1])
+                nc.gpsimd.tensor_tensor(out=b2_term[:, feats], in0=b2_term[:, feats], in1=h_sb[:, feats], op=ADD)
+
+        out_banks = {}
+
+        def second_layer_products(j, f):
+            nodes = slice(j * NODES, (j + 1) * NODES)
+            feats = slice(f * BANK, (f + 1) * BANK)
+            out_bank = psum_short.tile([P, BANK], F32, name="out_bank", tag="short")
+            for g in range(PASSES):
+                nc.tensor.matmul_mx(
+                    out=out_bank[:],
+                    lhsT=r_codes[:, g, nodes].bitcast(FP8X4),
+                    lhsT_scale=r_scales[:, g, nodes],
+                    rhs=w_codes[:, M2_CHUNK + g, feats].bitcast(FP8X4),
+                    rhs_scale=w_scales[:, M2_CHUNK + g, feats],
+                    start=(g == 0),
+                    stop=(g == PASSES - 1),
                 )
+            out_banks[(j, f)] = out_bank
 
-        def second_layer(c):
-            for j in range(c * J_TILE, (c + 1) * J_TILE):
-                nodes = slice(j * NODES, (j + 1) * NODES)
-                for f in range(HALVES):
-                    feats = slice(f * BANK, (f + 1) * BANK)
-                    out_bank = psum.tile([P, BANK], F32, name="out_bank", tag="bank")
-                    for g in range(PASSES):
-                        nc.tensor.matmul_mx(
-                            out=out_bank[:],
-                            lhsT=r_codes[:, g, nodes].bitcast(FP8X4),
-                            lhsT_scale=r_scales[:, g, nodes],
-                            rhs=w_codes[:, M2_CHUNK + g, feats].bitcast(FP8X4),
-                            rhs_scale=w_scales[:, M2_CHUNK + g, feats],
-                            start=(g == 0),
-                            stop=(g == PASSES - 1),
-                        )
-                    nc.vector.scalar_tensor_tensor(
-                        out=acc[:, feats],
-                        in0=out_bank[:],
-                        scalar=mask[:, j : j + 1],
-                        in1=acc[:, feats],
-                        op0=MULT,
-                        op1=ADD,
-                    )
+        def second_layer_sum(j, f):
+            feats = slice(f * BANK, (f + 1) * BANK)
+            so_far = b2_term if j == 0 else acc
+            nc.vector.scalar_tensor_tensor(
+                out=acc[:, feats],
+                in0=out_banks[(j, f)][:],
+                scalar=mask[:, j : j + 1],
+                in1=so_far[:, feats],
+                op0=MULT,
+                op1=ADD,
+            )
 
-        h_bank = psum.tile([P, PASSES, 2, NODES], F32, name="h_bank", tag="bank")
+        h_bank = psum_short.tile([P, PASSES, 2, NODES], F32, name="h_bank", tag="short")
         for g in range(PASSES):
             for u in range(2):
                 transpose_words(h_bank[:, g, u, :], h_sb[:], g, u)
         h_grouped = keep.tile([P, PASSES, BANK * PACK], BF16, align_bytes=64)
         for g in range(PASSES):
-            nc.vector.tensor_copy(
+            copy = nc.vector.tensor_copy if g == 0 else nc.scalar.copy
+            copy(
                 out=h_grouped[:, g, :].bitcast(F32).rearrange("p (x n u) -> p x n u", x=J_TILE, u=2),
                 in_=h_bank[:, g, :, :].rearrange("p u n -> p n u").unsqueeze(1).to_broadcast([P, J_TILE, NODES, 2]),
             )
-        b1_bank = psum.tile([P, P], BF16, name="b1_bank", tag="bank")
+        b1_bank = psum_short.tile([P, P], BF16, name="b1_bank", tag="short")
         nc.tensor.transpose(b1_bank[:], b1_rows[:], ident_bf16[:])
+
+        regroup_weights(XI_CHUNK, 0, W1_VECTOR_COLS)
         nc.vector.tensor_copy(out=b1[:], in_=b1_bank[:, 0:BLOCKS])
         for g in range(PASSES):
             nc.vector.quantize_mx(
                 out=h_codes[:, g, :].bitcast(FP8X4), scales=h_scales[:, g, :], in_=h_grouped[:, g, :]
             )
-
-        spread_b2()
-
-        quantise_w1_pieces(0, XI_CHUNK, E2_CHUNK, W1_VECTOR_COLS)
-        start_sum()
+        regroup_weights(XI_CHUNK + 1, 0, W1_VECTOR_COLS)
+        quantise_weights(XI_CHUNK, 0)
+        quantise_weights(XI_CHUNK + 1, 0)
+        transpose_edges(0, range(4))
+        target_products(0, 0, range(PACK))
+        regroup_weights(XJ_CHUNK, 0, W1_VECTOR_COLS)
+        regroup_weights(XJ_CHUNK + 1, 0, W1_VECTOR_COLS)
+        for g in range(PASSES):
+            quantise_edges(0, g)
+        quantise_weights(XJ_CHUNK, 0)
+        regroup_weights(E2_CHUNK, 0, W1_VECTOR_COLS)
+        quantise_weights(XJ_CHUNK + 1, 0)
+        regroup_weights(E2_CHUNK + 1, 0, W1_VECTOR_COLS)
+        transpose_edges(1, range(0, 2))
+        source_term_products(0)
         keep_source_term(0)
-        transpose_edges(0)
-        quantise_w1_pieces(0, E2_CHUNK, M2_CHUNK, BANK)
-        target_products(0, 0)
-        quantise_edges(0)
-        transpose_edges(1)
-        edge_products(0, 0)
+        transpose_edges(1, range(2, 4))
+        quantise_weights(E2_CHUNK, 0)
+        quantise_weights(E2_CHUNK + 1, 0)
+        edge_products(0, 0, range(PACK))
+        target_products(0, 1, range(0, 2))
 
         steps = [(g, c) for g in range(PASSES) for c in range(COL_TILES)]
-        node_pieces = [(chunk, 1) for chunk in range(XI_CHUNK, E2_CHUNK)]
-        edge_pieces = [(chunk, 1) for chunk in range(E2_CHUNK, M2_CHUNK)]
-        m2_pieces = [(M2_CHUNK + g, half) for g in range(PASSES) for half in range(HALVES)]
-
-        def regroup_in_round(n, round_of_pieces, pieces, vector_cols):
-            if n == round_of_pieces:
-                for chunk, half in pieces:
-                    regroup_weights(chunk, half, vector_cols)
-
-        def quantise_in_round(n, round_of_pieces, pieces):
-            if n == round_of_pieces + 1:
-                for chunk, half in pieces:
-                    quantise_weights(chunk, half)
-
-        for n in range(len(steps) + 2):
-            if 1 <= n <= len(steps):
-                first_layer_relu(steps[n - 1][0], steps[n - 1][1])
-            if n >= 2:
-                quantise_hidden(steps[n - 2][0], steps[n - 2][1])
-            regroup_in_round(n, NODE_WEIGHTS_ROUND, node_pieces, LATE_VECTOR_COLS)
-            regroup_in_round(n, EDGE_WEIGHTS_ROUND, edge_pieces, LATE_VECTOR_COLS)
-            for number, piece in enumerate(m2_pieces):
-                regroup_in_round(n, M2_ROUND + number, [piece], 0)
-            if n < len(steps):
-                first_layer_sums(steps[n][0], steps[n][1])
-            quantise_in_round(n, NODE_WEIGHTS_ROUND, node_pieces)
-            quantise_in_round(n, EDGE_WEIGHTS_ROUND, edge_pieces)
-            for number, piece in enumerate(m2_pieces):
-                quantise_in_round(n, M2_ROUND + number, [piece])
-            if n == NODE_WEIGHTS_ROUND + 1:
-                source_term_products(1)
-            if n >= 2 and steps[n - 2][0] == PASSES - 1:
-                second_layer(steps[n - 2][1])
-            if n + 2 < COL_TILES:
-                transpose_edges(n + 2)
-            if n + 1 < len(steps):
-                target_products(steps[n + 1][0], steps[n + 1][1])
+        regroup_rounds = [
+            [(XI_CHUNK, 1), (XI_CHUNK + 1, 1)],
+            [(XJ_CHUNK, 1), (XJ_CHUNK + 1, 1), (E2_CHUNK, 1), (E2_CHUNK + 1, 1)],
+            [(M2_CHUNK, 0), (M2_CHUNK + 1, 0)],
+            [(M2_CHUNK, 1), (M2_CHUNK + 1, 1)],
+        ]
+        to_multiply = []
+        to_sum = []
+        for n in range(len(steps) + QUANT_DELAY + 1):
+            if n == 1:
+                start_sum()
+            vector_work = []
             if n + 1 < COL_TILES:
-                quantise_edges(n + 1)
-            if n == NODE_WEIGHTS_ROUND + 1:
+                vector_work.extend([(quantise_edges, (n + 1, g)) for g in range(PASSES)])
+            if 0 <= n - QUANT_DELAY < len(steps):
+                vector_work.append((quantise_hidden, steps[n - QUANT_DELAY]))
+            if 1 <= n <= len(regroup_rounds):
+                vector_work.extend([(quantise_weights, piece) for piece in regroup_rounds[n - 1]])
+            if n == 3:
+                source_term_products(1)
                 keep_source_term(1)
-            if n + 1 < len(steps):
-                edge_products(steps[n + 1][0], steps[n + 1][1])
+            scalar_work = []
+            if 0 <= n - RELU_DELAY < len(steps):
+                scalar_work.append((first_layer_relu, steps[n - RELU_DELAY]))
+            if n < len(regroup_rounds):
+                for chunk, half in regroup_rounds[n]:
+                    scalar_work.append((regroup_weights, (chunk, half, LATE_VECTOR_COLS if chunk < M2_CHUNK else 0)))
+            for t in range(PACK):
+                if n + 2 < COL_TILES and t % 2 == 0:
+                    transpose_edges(n + 2, range(t, t + 2))
+                if t % 2 == 0:
+                    for number in range((len(scalar_work) + 1) // 2 if t == 0 else len(scalar_work)):
+                        work, arguments = scalar_work.pop(0)
+                        work(*arguments)
+                multiplied = to_multiply[:2]
+                to_multiply = to_multiply[2:]
+                for j, f in multiplied:
+                    second_layer_products(j, f)
+                if n < len(steps):
+                    first_layer_sum(steps[n][0], steps[n][1], t)
+                for _ in range(PASSES if t == 0 else 1):
+                    if vector_work:
+                        work, arguments = vector_work.pop(0)
+                        work(*arguments)
+                for j, f in to_sum:
+                    second_layer_sum(j, f)
+                to_sum = multiplied
+                if n + 1 < len(steps):
+                    g, c = steps[n + 1]
+                    if n > 0 or t >= 2:
+                        target_products(g, c, [t])
+                    if n > 0:
+                        edge_products(g, c, [t])
+                    elif t == PACK - 1:
+                        edge_products(g, c, range(PACK))
+            for work, arguments in vector_work:
+                work(*arguments)
+            if 0 <= n - QUANT_DELAY < len(steps):
+                g, c = steps[n - QUANT_DELAY]
+                if g == PASSES - 1:
+                    to_multiply.extend([(j, f) for j in range(c * J_TILE, (c + 1) * J_TILE) for f in range(HALVES)])
+        for j, f in to_sum:
+            second_layer_sum(j, f)
 
         for f in range(HALVES):
             feats = slice(f * BANK, (f + 1) * BANK)

@@ -7,6 +7,7 @@ FP8X4 = mybir.dt.float8_e4m3fn_x4
 BF16 = mybir.dt.bfloat16
 F32 = mybir.dt.float32
 U32 = mybir.dt.uint32
+I32 = mybir.dt.int32
 U8 = mybir.dt.uint8
 ADD = mybir.AluOpType.add
 MULT = mybir.AluOpType.mult
@@ -33,8 +34,11 @@ RUN = 4
 XI_CHUNK, XJ_CHUNK, E2_CHUNK, M2_CHUNK = 0, 2, 4, 6
 WEIGHT_CHUNKS = 8
 W1_VECTOR_COLS = BANK // 2
-LATE_VECTOR_COLS = 3 * BANK // 4
-RELU_DELAY, QUANT_DELAY = 2, 3
+XJ_VECTOR_COLS = 3 * BANK // 4
+LATE_VECTOR_COLS = 5 * BANK // 8
+SIDE_TILES, SIDE_NODES = 2, (1, 3)
+START_SUM_ROUND = 6
+RELU_DELAY, QUANT_DELAY = 1, 2
 
 FLOPS = 2 * WIDTH * WIDTH * (2 * NODES + 2 * EDGES)
 
@@ -50,7 +54,7 @@ def tile_messagepassing_pa_kernel(tc, h, e, adj_mask, W_m1, b_m1, W_m2, b_m2, ou
         keep = stack.enter_context(tc.tile_pool(name="keep", bufs=1))
         raw_pool = stack.enter_context(tc.tile_pool(name="raw", bufs=6))
         edge_pool = stack.enter_context(tc.tile_pool(name="edge", bufs=3))
-        grouped_pool = stack.enter_context(tc.tile_pool(name="grouped", bufs=6))
+        grouped_pool = stack.enter_context(tc.tile_pool(name="grouped", bufs=3))
         stage = stack.enter_context(tc.tile_pool(name="stage", bufs=3))
         psum = stack.enter_context(tc.psum_pool(name="psum", bufs=5))
         psum_short = stack.enter_context(tc.psum_pool(name="psum_short", bufs=3))
@@ -115,12 +119,12 @@ def tile_messagepassing_pa_kernel(tc, h, e, adj_mask, W_m1, b_m1, W_m2, b_m2, ou
         ones = keep.tile([P, P], BF16)
         nc.vector.memset(ones[:], 1.0)
 
-        w_codes = keep.tile([P, WEIGHT_CHUNKS, WIDTH], U32, align_bytes=64)
-        w_scales = keep.tile([P, WEIGHT_CHUNKS, WIDTH], U8, align_bytes=64)
+        w_codes = keep.tile([P, HALVES, WEIGHT_CHUNKS, BANK], U32, align_bytes=64)
+        w_scales = keep.tile([P, HALVES, WEIGHT_CHUNKS, BANK], U8, align_bytes=64)
         h_codes = keep.tile([P, PASSES, BANK], U32, align_bytes=64)
         h_scales = keep.tile([P, PASSES, BANK], U8, align_bytes=64)
-        e_codes = keep.tile([P, PASSES, EDGES], U32, align_bytes=64)
-        e_scales = keep.tile([P, PASSES, EDGES], U8, align_bytes=64)
+        e_codes = keep.tile([P, COL_TILES, PASSES, BANK], U32, align_bytes=64)
+        e_scales = keep.tile([P, COL_TILES, PASSES, BANK], U8, align_bytes=64)
         r_codes = keep.tile([P, PASSES, EDGES], U32, align_bytes=64)
         r_scales = keep.tile([P, PASSES, EDGES], U8, align_bytes=64)
 
@@ -130,23 +134,28 @@ def tile_messagepassing_pa_kernel(tc, h, e, adj_mask, W_m1, b_m1, W_m2, b_m2, ou
                 in_=raw[:, :, cols].rearrange("p t (c i) -> p c t i", i=RUN),
             )
 
-        grouped_pieces = {}
+        grouped_pairs = {}
 
         def regroup_weights(chunk, half, vector_cols):
             raw = raw_pieces[(chunk, half)]
-            grouped = grouped_pool.tile([P, BANK, PACK], BF16, name="grouped", tag="grouped", align_bytes=64)
+            pair, member = chunk // PASSES, chunk % PASSES
+            if member == 0:
+                grouped_pairs[(pair, half)] = grouped_pool.tile(
+                    [P, PASSES, BANK, PACK], BF16, name="grouped", tag="grouped", align_bytes=64
+                )
+            grouped = grouped_pairs[(pair, half)][:, member, :, :]
             if vector_cols > 0:
                 regroup(nc.vector.tensor_copy, grouped, raw, slice(0, vector_cols))
             if vector_cols < BANK:
                 regroup(nc.scalar.copy, grouped, raw, slice(vector_cols, BANK))
-            grouped_pieces[(chunk, half)] = grouped
 
-        def quantise_weights(chunk, half):
-            cols = slice(half * BANK, (half + 1) * BANK)
+        def quantise_weights(first_chunk, chunks, half):
+            chunk_range = slice(first_chunk, first_chunk + chunks)
+            members = slice(first_chunk % PASSES, first_chunk % PASSES + chunks)
             nc.vector.quantize_mx(
-                out=w_codes[:, chunk, cols].bitcast(FP8X4),
-                scales=w_scales[:, chunk, cols],
-                in_=grouped_pieces[(chunk, half)][:].rearrange("p n t -> p (n t)"),
+                out=w_codes[:, half, chunk_range, :].rearrange("p c n -> p (c n)").bitcast(FP8X4),
+                scales=w_scales[:, half, chunk_range, :].rearrange("p c n -> p (c n)"),
+                in_=grouped_pairs[(first_chunk // PASSES, half)][:, members, :, :].rearrange("p c n t -> p (c n t)"),
             )
 
         def transpose_words(bank_cols, rows_bf16, g, u):
@@ -160,12 +169,12 @@ def tile_messagepassing_pa_kernel(tc, h, e, adj_mask, W_m1, b_m1, W_m2, b_m2, ou
         def source_term_products(half):
             bank = psum_short.tile([P, PACK, NODES], F32, name="source_bank", tag="short")
             for t in range(PACK):
-                units = slice((PACK * half + t) * P, (PACK * half + t + 1) * P)
+                units = slice(t * P, (t + 1) * P)
                 for kp in range(PASSES):
                     nc.tensor.matmul_mx(
                         out=bank[:, t, :],
-                        lhsT=w_codes[:, XJ_CHUNK + kp, units].bitcast(FP8X4),
-                        lhsT_scale=w_scales[:, XJ_CHUNK + kp, units],
+                        lhsT=w_codes[:, half, XJ_CHUNK + kp, units].bitcast(FP8X4),
+                        lhsT_scale=w_scales[:, half, XJ_CHUNK + kp, units],
                         rhs=h_codes[:, kp, 0:NODES].bitcast(FP8X4),
                         rhs_scale=h_scales[:, kp, 0:NODES],
                         start=(kp == 0),
@@ -185,11 +194,11 @@ def tile_messagepassing_pa_kernel(tc, h, e, adj_mask, W_m1, b_m1, W_m2, b_m2, ou
         def transpose_edges(c, banks):
             for number in banks:
                 g, first_j = number // 2, 2 * (number % 2)
-                if first_j == 0:
-                    e_grouped_tiles[(c, g)] = stage.tile(
-                        [P, BANK * PACK], BF16, name="e_grouped", tag="e_grouped", bufs=4, align_bytes=64
+                if number == 0:
+                    e_grouped_tiles[c] = stage.tile(
+                        [P, PASSES, BANK * PACK], BF16, name="e_grouped", tag="e_grouped", bufs=2, align_bytes=64
                     )
-                e_words = e_grouped_tiles[(c, g)][:].bitcast(F32).rearrange("p (x n u) -> p x n u", x=J_TILE, u=2)
+                e_words = e_grouped_tiles[c][:, g, :].bitcast(F32).rearrange("p (x n u) -> p x n u", x=J_TILE, u=2)
                 e_bank = psum_short.tile([P, 2, 2, NODES], F32, name="e_bank", tag="short")
                 for x in range(2):
                     for u in range(2):
@@ -199,12 +208,11 @@ def tile_messagepassing_pa_kernel(tc, h, e, adj_mask, W_m1, b_m1, W_m2, b_m2, ou
                     in_=e_bank[:].rearrange("p x u n -> p x n u"),
                 )
 
-        def quantise_edges(c, g):
-            cols = slice(c * BANK, (c + 1) * BANK)
+        def quantise_edges(c):
             nc.vector.quantize_mx(
-                out=e_codes[:, g, cols].bitcast(FP8X4),
-                scales=e_scales[:, g, cols],
-                in_=e_grouped_tiles[(c, g)][:],
+                out=e_codes[:, c, :, :].rearrange("p g n -> p (g n)").bitcast(FP8X4),
+                scales=e_scales[:, c, :, :].rearrange("p g n -> p (g n)"),
+                in_=e_grouped_tiles[c][:].rearrange("p g k -> p (g k)"),
             )
 
         edge_banks = {}
@@ -213,13 +221,13 @@ def tile_messagepassing_pa_kernel(tc, h, e, adj_mask, W_m1, b_m1, W_m2, b_m2, ou
 
         def target_products(g, c, blocks):
             for t in blocks:
-                units = slice((PACK * g + t) * P, (PACK * g + t + 1) * P)
+                units = slice(t * P, (t + 1) * P)
                 edge_bank = psum.tile([P, BANK], F32, name="edge_bank", tag="bank")
                 for kp in range(PASSES):
                     nc.tensor.matmul_mx(
                         out=edge_bank[:],
-                        lhsT=w_codes[:, XI_CHUNK + kp, units].bitcast(FP8X4),
-                        lhsT_scale=w_scales[:, XI_CHUNK + kp, units],
+                        lhsT=w_codes[:, g, XI_CHUNK + kp, units].bitcast(FP8X4),
+                        lhsT_scale=w_scales[:, g, XI_CHUNK + kp, units],
                         rhs=h_codes[:, kp, :].bitcast(FP8X4),
                         rhs_scale=h_scales[:, kp, :],
                         start=(kp == 0),
@@ -228,16 +236,15 @@ def tile_messagepassing_pa_kernel(tc, h, e, adj_mask, W_m1, b_m1, W_m2, b_m2, ou
                 edge_banks[(g, c, t)] = edge_bank
 
         def edge_products(g, c, blocks):
-            cols = slice(c * BANK, (c + 1) * BANK)
             for t in blocks:
-                units = slice((PACK * g + t) * P, (PACK * g + t + 1) * P)
+                units = slice(t * P, (t + 1) * P)
                 for kp in range(PASSES):
                     nc.tensor.matmul_mx(
                         out=edge_banks[(g, c, t)][:],
-                        lhsT=w_codes[:, E2_CHUNK + kp, units].bitcast(FP8X4),
-                        lhsT_scale=w_scales[:, E2_CHUNK + kp, units],
-                        rhs=e_codes[:, kp, cols].bitcast(FP8X4),
-                        rhs_scale=e_scales[:, kp, cols],
+                        lhsT=w_codes[:, g, E2_CHUNK + kp, units].bitcast(FP8X4),
+                        lhsT_scale=w_scales[:, g, E2_CHUNK + kp, units],
+                        rhs=e_codes[:, c, kp, :].bitcast(FP8X4),
+                        rhs_scale=e_scales[:, c, kp, :],
                         start=False,
                         stop=(kp == PASSES - 1),
                     )
@@ -275,7 +282,8 @@ def tile_messagepassing_pa_kernel(tc, h, e, adj_mask, W_m1, b_m1, W_m2, b_m2, ou
         mask = keep.tile([P, GRAPH_NODES], F32)
         mask_sum = keep.tile([P, 1], F32)
         acc = keep.tile([P, WIDTH], F32)
-        b2_term = keep.tile([P, WIDTH], F32)
+        side = keep.tile([P, WIDTH], F32)
+        scaled_pool = stack.enter_context(tc.tile_pool(name="scaled", bufs=3))
         nc.vector.tensor_copy(out=mask[:], in_=mask_bf16[:])
         nc.vector.tensor_reduce(out=mask_sum[:], in_=mask[:], axis=mybir.AxisListType.X, op=ADD)
 
@@ -284,22 +292,20 @@ def tile_messagepassing_pa_kernel(tc, h, e, adj_mask, W_m1, b_m1, W_m2, b_m2, ou
                 feats = slice(f * BANK, (f + 1) * BANK)
                 b2_bank = psum_short.tile([P, BANK], F32, name="b2_bank", tag="short")
                 nc.tensor.matmul(out=b2_bank[:], lhsT=ones[:], rhs=b2_row[:, feats], start=True, stop=True)
-                nc.scalar.activation(out=b2_term[:, feats], in_=b2_bank[:], func=COPY, scale=mask_sum[:, 0:1])
-                nc.gpsimd.tensor_tensor(out=b2_term[:, feats], in0=b2_term[:, feats], in1=h_sb[:, feats], op=ADD)
+                nc.scalar.activation(out=side[:, feats], in_=b2_bank[:], func=COPY, scale=mask_sum[:, 0:1])
 
         out_banks = {}
 
         def second_layer_products(j, f):
             nodes = slice(j * NODES, (j + 1) * NODES)
-            feats = slice(f * BANK, (f + 1) * BANK)
-            out_bank = psum_short.tile([P, BANK], F32, name="out_bank", tag="short")
+            out_bank = psum.tile([P, BANK], F32, name="out_bank", tag="bank")
             for g in range(PASSES):
                 nc.tensor.matmul_mx(
                     out=out_bank[:],
                     lhsT=r_codes[:, g, nodes].bitcast(FP8X4),
                     lhsT_scale=r_scales[:, g, nodes],
-                    rhs=w_codes[:, M2_CHUNK + g, feats].bitcast(FP8X4),
-                    rhs_scale=w_scales[:, M2_CHUNK + g, feats],
+                    rhs=w_codes[:, f, M2_CHUNK + g, :].bitcast(FP8X4),
+                    rhs_scale=w_scales[:, f, M2_CHUNK + g, :],
                     start=(g == 0),
                     stop=(g == PASSES - 1),
                 )
@@ -307,7 +313,18 @@ def tile_messagepassing_pa_kernel(tc, h, e, adj_mask, W_m1, b_m1, W_m2, b_m2, ou
 
         def second_layer_sum(j, f):
             feats = slice(f * BANK, (f + 1) * BANK)
-            so_far = b2_term if j == 0 else acc
+            c, x = j // J_TILE, j % J_TILE
+            if c < SIDE_TILES and x in SIDE_NODES:
+                scaled = scaled_pool.tile([P, BANK], F32, name="scaled", tag="scaled")
+                nc.scalar.activation(out=scaled[:], in_=out_banks[(j, f)][:], func=COPY, scale=mask[:, j : j + 1])
+                nc.gpsimd.tensor_tensor(out=side[:, feats], in0=side[:, feats], in1=scaled[:], op=ADD)
+                return
+            so_far = acc
+            if j == 0:
+                so_far = h_sb
+            if c == COL_TILES - 1 and x == 0:
+                nc.gpsimd.tensor_tensor(out=side[:, feats], in0=side[:, feats], in1=acc[:, feats], op=ADD)
+                so_far = side
             nc.vector.scalar_tensor_tensor(
                 out=acc[:, feats],
                 in0=out_banks[(j, f)][:],
@@ -321,13 +338,11 @@ def tile_messagepassing_pa_kernel(tc, h, e, adj_mask, W_m1, b_m1, W_m2, b_m2, ou
         for g in range(PASSES):
             for u in range(2):
                 transpose_words(h_bank[:, g, u, :], h_sb[:], g, u)
-        h_grouped = keep.tile([P, PASSES, BANK * PACK], BF16, align_bytes=64)
-        for g in range(PASSES):
-            copy = nc.vector.tensor_copy if g == 0 else nc.scalar.copy
-            copy(
-                out=h_grouped[:, g, :].bitcast(F32).rearrange("p (x n u) -> p x n u", x=J_TILE, u=2),
-                in_=h_bank[:, g, :, :].rearrange("p u n -> p n u").unsqueeze(1).to_broadcast([P, J_TILE, NODES, 2]),
-            )
+        h_grouped = keep.tile([P, PASSES, NODES * PACK], BF16, align_bytes=64)
+        nc.scalar.copy(
+            out=h_grouped[:].rearrange("p g k -> p (g k)").bitcast(F32).rearrange("p (g n u) -> p g n u", g=PASSES, u=2),
+            in_=h_bank[:].rearrange("p g u n -> p g n u"),
+        )
         b1_bank = psum_short.tile([P, P], BF16, name="b1_bank", tag="short")
         nc.tensor.transpose(b1_bank[:], b1_rows[:], ident_bf16[:])
 
@@ -335,81 +350,98 @@ def tile_messagepassing_pa_kernel(tc, h, e, adj_mask, W_m1, b_m1, W_m2, b_m2, ou
         nc.vector.tensor_copy(out=b1[:], in_=b1_bank[:, 0:BLOCKS])
         for g in range(PASSES):
             nc.vector.quantize_mx(
-                out=h_codes[:, g, :].bitcast(FP8X4), scales=h_scales[:, g, :], in_=h_grouped[:, g, :]
+                out=h_codes[:, g, 0:NODES].bitcast(FP8X4), scales=h_scales[:, g, 0:NODES], in_=h_grouped[:, g, :]
+            )
+        for width in (NODES, 2 * NODES):
+            nc.vector.tensor_copy(
+                out=h_codes[:].bitcast(I32)[:, :, width : 2 * width], in_=h_codes[:].bitcast(I32)[:, :, 0:width]
+            )
+            words = width // PACK
+            nc.vector.tensor_copy(
+                out=h_scales[:].bitcast(I32)[:, :, words : 2 * words], in_=h_scales[:].bitcast(I32)[:, :, 0:words]
             )
         regroup_weights(XI_CHUNK + 1, 0, W1_VECTOR_COLS)
-        quantise_weights(XI_CHUNK, 0)
-        quantise_weights(XI_CHUNK + 1, 0)
+        quantise_weights(XI_CHUNK, 1, 0)
+        quantise_weights(XI_CHUNK + 1, 1, 0)
         transpose_edges(0, range(4))
         target_products(0, 0, range(PACK))
-        regroup_weights(XJ_CHUNK, 0, W1_VECTOR_COLS)
-        regroup_weights(XJ_CHUNK + 1, 0, W1_VECTOR_COLS)
-        for g in range(PASSES):
-            quantise_edges(0, g)
-        quantise_weights(XJ_CHUNK, 0)
+        regroup_weights(XJ_CHUNK, 0, XJ_VECTOR_COLS)
+        regroup_weights(XJ_CHUNK + 1, 0, XJ_VECTOR_COLS)
+        quantise_edges(0)
         regroup_weights(E2_CHUNK, 0, W1_VECTOR_COLS)
-        quantise_weights(XJ_CHUNK + 1, 0)
+        quantise_weights(XJ_CHUNK, 1, 0)
         regroup_weights(E2_CHUNK + 1, 0, W1_VECTOR_COLS)
+        quantise_weights(XJ_CHUNK + 1, 1, 0)
         transpose_edges(1, range(0, 2))
         source_term_products(0)
         keep_source_term(0)
         transpose_edges(1, range(2, 4))
-        quantise_weights(E2_CHUNK, 0)
-        quantise_weights(E2_CHUNK + 1, 0)
+        quantise_weights(E2_CHUNK, 1, 0)
+        quantise_weights(E2_CHUNK + 1, 1, 0)
         edge_products(0, 0, range(PACK))
-        target_products(0, 1, range(0, 2))
+        target_products(0, 1, range(0, 1))
 
         steps = [(g, c) for g in range(PASSES) for c in range(COL_TILES)]
-        regroup_rounds = [
-            [(XI_CHUNK, 1), (XI_CHUNK + 1, 1)],
-            [(XJ_CHUNK, 1), (XJ_CHUNK + 1, 1), (E2_CHUNK, 1), (E2_CHUNK + 1, 1)],
-            [(M2_CHUNK, 0), (M2_CHUNK + 1, 0)],
-            [(M2_CHUNK, 1), (M2_CHUNK + 1, 1)],
-        ]
+        regroup_rounds = {
+            0: [(XI_CHUNK, 1), (XI_CHUNK + 1, 1)],
+            1: [(XJ_CHUNK, 1), (XJ_CHUNK + 1, 1), (E2_CHUNK, 1), (E2_CHUNK + 1, 1)],
+            2: [(M2_CHUNK, 0)],
+            3: [(M2_CHUNK + 1, 0)],
+            4: [(M2_CHUNK, 1)],
+            5: [(M2_CHUNK + 1, 1)],
+        }
         to_multiply = []
         to_sum = []
         for n in range(len(steps) + QUANT_DELAY + 1):
-            if n == 1:
+            if n == START_SUM_ROUND:
                 start_sum()
             vector_work = []
             if n + 1 < COL_TILES:
-                vector_work.extend([(quantise_edges, (n + 1, g)) for g in range(PASSES)])
+                vector_work.append((quantise_edges, (n + 1,)))
             if 0 <= n - QUANT_DELAY < len(steps):
                 vector_work.append((quantise_hidden, steps[n - QUANT_DELAY]))
-            if 1 <= n <= len(regroup_rounds):
-                vector_work.extend([(quantise_weights, piece) for piece in regroup_rounds[n - 1]])
-            if n == 3:
+            for chunk, half in regroup_rounds.get(n - 1, []):
+                if chunk % PASSES == PASSES - 1:
+                    vector_work.append((quantise_weights, (chunk - 1, PASSES, half)))
+            scalar_work = []
+            for chunk, half in regroup_rounds.get(n, []):
+                scalar_work.append((regroup_weights, (chunk, half, LATE_VECTOR_COLS if chunk < M2_CHUNK else 0)))
+            if 0 <= n - RELU_DELAY < len(steps):
+                scalar_work.insert(len(scalar_work) if n >= 2 else 0, (first_layer_relu, steps[n - RELU_DELAY]))
+            if n == COL_TILES - 1:
+                work, arguments = scalar_work.pop(0)
+                work(*arguments)
                 source_term_products(1)
                 keep_source_term(1)
-            scalar_work = []
-            if 0 <= n - RELU_DELAY < len(steps):
-                scalar_work.append((first_layer_relu, steps[n - RELU_DELAY]))
-            if n < len(regroup_rounds):
-                for chunk, half in regroup_rounds[n]:
-                    scalar_work.append((regroup_weights, (chunk, half, LATE_VECTOR_COLS if chunk < M2_CHUNK else 0)))
             for t in range(PACK):
-                if n + 2 < COL_TILES and t % 2 == 0:
-                    transpose_edges(n + 2, range(t, t + 2))
                 if t % 2 == 0:
-                    for number in range((len(scalar_work) + 1) // 2 if t == 0 else len(scalar_work)):
-                        work, arguments = scalar_work.pop(0)
-                        work(*arguments)
+                    if n + 2 < COL_TILES:
+                        for number in range(n + 1 if t == 0 else 1):
+                            work, arguments = scalar_work.pop(0)
+                            work(*arguments)
+                        transpose_edges(n + 2, range(t, t + 2))
+                        for number in range(min(n, len(scalar_work))):
+                            work, arguments = scalar_work.pop(0)
+                            work(*arguments)
+                    else:
+                        for number in range((len(scalar_work) + 1) // 2 if t == 0 else len(scalar_work)):
+                            work, arguments = scalar_work.pop(0)
+                            work(*arguments)
                 multiplied = to_multiply[:2]
                 to_multiply = to_multiply[2:]
                 for j, f in multiplied:
                     second_layer_products(j, f)
                 if n < len(steps):
                     first_layer_sum(steps[n][0], steps[n][1], t)
-                for _ in range(PASSES if t == 0 else 1):
-                    if vector_work:
-                        work, arguments = vector_work.pop(0)
-                        work(*arguments)
+                if vector_work:
+                    work, arguments = vector_work.pop(0)
+                    work(*arguments)
                 for j, f in to_sum:
                     second_layer_sum(j, f)
                 to_sum = multiplied
                 if n + 1 < len(steps):
                     g, c = steps[n + 1]
-                    if n > 0 or t >= 2:
+                    if n > 0 or t >= 1:
                         target_products(g, c, [t])
                     if n > 0:
                         edge_products(g, c, [t])
@@ -420,7 +452,7 @@ def tile_messagepassing_pa_kernel(tc, h, e, adj_mask, W_m1, b_m1, W_m2, b_m2, ou
             if 0 <= n - QUANT_DELAY < len(steps):
                 g, c = steps[n - QUANT_DELAY]
                 if g == PASSES - 1:
-                    to_multiply.extend([(j, f) for j in range(c * J_TILE, (c + 1) * J_TILE) for f in range(HALVES)])
+                    to_multiply.extend([(j, f) for f in range(HALVES) for j in range(c * J_TILE, (c + 1) * J_TILE)])
         for j, f in to_sum:
             second_layer_sum(j, f)
 

@@ -36,7 +36,7 @@ WEIGHT_CHUNKS = 8
 W1_VECTOR_COLS = BANK // 2
 XJ_VECTOR_COLS = 3 * BANK // 4
 LATE_VECTOR_COLS = 5 * BANK // 8
-SIDE_TILES, SIDE_NODES = 2, (1, 3)
+SIDE_NODE = 1
 START_SUM_ROUND = 6
 RELU_DELAY, QUANT_DELAY = 1, 2
 
@@ -314,7 +314,7 @@ def tile_messagepassing_pa_kernel(tc, h, e, adj_mask, W_m1, b_m1, W_m2, b_m2, ou
         def second_layer_sum(j, f):
             feats = slice(f * BANK, (f + 1) * BANK)
             c, x = j // J_TILE, j % J_TILE
-            if c < SIDE_TILES and x in SIDE_NODES:
+            if x == SIDE_NODE:
                 scaled = scaled_pool.tile([P, BANK], F32, name="scaled", tag="scaled")
                 nc.scalar.activation(out=scaled[:], in_=out_banks[(j, f)][:], func=COPY, scale=mask[:, j : j + 1])
                 nc.gpsimd.tensor_tensor(out=side[:, feats], in0=side[:, feats], in1=scaled[:], op=ADD)
@@ -322,9 +322,6 @@ def tile_messagepassing_pa_kernel(tc, h, e, adj_mask, W_m1, b_m1, W_m2, b_m2, ou
             so_far = acc
             if j == 0:
                 so_far = h_sb
-            if c == COL_TILES - 1 and x == 0:
-                nc.gpsimd.tensor_tensor(out=side[:, feats], in0=side[:, feats], in1=acc[:, feats], op=ADD)
-                so_far = side
             nc.vector.scalar_tensor_tensor(
                 out=acc[:, feats],
                 in0=out_banks[(j, f)][:],
@@ -452,10 +449,11 @@ def tile_messagepassing_pa_kernel(tc, h, e, adj_mask, W_m1, b_m1, W_m2, b_m2, ou
             if 0 <= n - QUANT_DELAY < len(steps):
                 g, c = steps[n - QUANT_DELAY]
                 if g == PASSES - 1:
-                    to_multiply.extend([(j, f) for f in range(HALVES) for j in range(c * J_TILE, (c + 1) * J_TILE)])
+                    to_multiply.extend([(j, f) for j in range(c * J_TILE, (c + 1) * J_TILE) for f in range(HALVES)])
         for j, f in to_sum:
             second_layer_sum(j, f)
 
         for f in range(HALVES):
             feats = slice(f * BANK, (f + 1) * BANK)
+            nc.vector.tensor_tensor(out=acc[:, feats], in0=acc[:, feats], in1=side[:, feats], op=ADD)
             nc.sync.dma_start(out=out_rows[:, feats], in_=acc[:, feats])

@@ -33,12 +33,13 @@ RUN = 4
 
 XI_CHUNK, XJ_CHUNK, E2_CHUNK, M2_CHUNK = 0, 2, 4, 6
 WEIGHT_CHUNKS = 8
-W1_VECTOR_COLS = BANK // 2
-XJ_VECTOR_COLS = 3 * BANK // 4
-LATE_VECTOR_COLS = 5 * BANK // 8
+XI_VECTOR_COLS = BANK // 4
+EARLY_VECTOR_COLS = 3 * BANK // 4
+LATE_VECTOR_COLS = 3 * BANK // 8
+M2_VECTOR_COLS = BANK // 4
+IDLE_PRODUCTS = 4
 SIDE_NODE = 1
-START_SUM_ROUND = 6
-RELU_DELAY, QUANT_DELAY = 1, 2
+RELU_DELAY, QUANT_DELAY = 2, 3
 
 FLOPS = 2 * WIDTH * WIDTH * (2 * NODES + 2 * EDGES)
 
@@ -101,9 +102,11 @@ def tile_messagepassing_pa_kernel(tc, h, e, adj_mask, W_m1, b_m1, W_m2, b_m2, ou
         for chunk in range(XJ_CHUNK, M2_CHUNK):
             raw_pieces[(chunk, 0)] = load_w1_piece(chunk, 0)
         e_tiles.extend([load_edges(c) for c in range(1, COL_TILES - 1)])
-        for chunk in range(XI_CHUNK, M2_CHUNK):
+        for chunk in range(XI_CHUNK, E2_CHUNK):
             raw_pieces[(chunk, 1)] = load_w1_piece(chunk, 1)
         e_tiles.append(load_edges(COL_TILES - 1))
+        for chunk in range(E2_CHUNK, M2_CHUNK):
+            raw_pieces[(chunk, 1)] = load_w1_piece(chunk, 1)
         for half in range(HALVES):
             for g in range(PASSES):
                 raw_pieces[(M2_CHUNK + g, half)] = load_w2_piece(g, half)
@@ -136,18 +139,19 @@ def tile_messagepassing_pa_kernel(tc, h, e, adj_mask, W_m1, b_m1, W_m2, b_m2, ou
 
         grouped_pairs = {}
 
-        def regroup_weights(chunk, half, vector_cols):
-            raw = raw_pieces[(chunk, half)]
+        def grouped_piece(chunk, half):
             pair, member = chunk // PASSES, chunk % PASSES
-            if member == 0:
+            if (pair, half) not in grouped_pairs:
                 grouped_pairs[(pair, half)] = grouped_pool.tile(
                     [P, PASSES, BANK, PACK], BF16, name="grouped", tag="grouped", align_bytes=64
                 )
-            grouped = grouped_pairs[(pair, half)][:, member, :, :]
-            if vector_cols > 0:
-                regroup(nc.vector.tensor_copy, grouped, raw, slice(0, vector_cols))
-            if vector_cols < BANK:
-                regroup(nc.scalar.copy, grouped, raw, slice(vector_cols, BANK))
+            return grouped_pairs[(pair, half)][:, member, :, :]
+
+        def regroup_scalar_share(chunk, half, vector_cols):
+            regroup(nc.scalar.copy, grouped_piece(chunk, half), raw_pieces[(chunk, half)], slice(vector_cols, BANK))
+
+        def regroup_vector_share(chunk, half, vector_cols):
+            regroup(nc.vector.tensor_copy, grouped_piece(chunk, half), raw_pieces[(chunk, half)], slice(0, vector_cols))
 
         def quantise_weights(first_chunk, chunks, half):
             chunk_range = slice(first_chunk, first_chunk + chunks)
@@ -294,6 +298,11 @@ def tile_messagepassing_pa_kernel(tc, h, e, adj_mask, W_m1, b_m1, W_m2, b_m2, ou
                 nc.tensor.matmul(out=b2_bank[:], lhsT=ones[:], rhs=b2_row[:, feats], start=True, stop=True)
                 nc.scalar.activation(out=side[:, feats], in_=b2_bank[:], func=COPY, scale=mask_sum[:, 0:1])
 
+        def keep_tensor_busy():
+            idle_bank = psum_short.tile([P, BANK], F32, name="idle_bank", tag="short")
+            for number in range(IDLE_PRODUCTS):
+                nc.tensor.matmul(out=idle_bank[:], lhsT=ones[:], rhs=b2_row[:, 0:BANK], start=True, stop=True)
+
         out_banks = {}
 
         def second_layer_products(j, f):
@@ -343,7 +352,11 @@ def tile_messagepassing_pa_kernel(tc, h, e, adj_mask, W_m1, b_m1, W_m2, b_m2, ou
         b1_bank = psum_short.tile([P, P], BF16, name="b1_bank", tag="short")
         nc.tensor.transpose(b1_bank[:], b1_rows[:], ident_bf16[:])
 
-        regroup_weights(XI_CHUNK, 0, W1_VECTOR_COLS)
+        def regroup_weights(chunk, half, vector_cols):
+            regroup_scalar_share(chunk, half, vector_cols)
+            regroup_vector_share(chunk, half, vector_cols)
+
+        regroup_weights(XI_CHUNK, 0, XI_VECTOR_COLS)
         nc.vector.tensor_copy(out=b1[:], in_=b1_bank[:, 0:BLOCKS])
         for g in range(PASSES):
             nc.vector.quantize_mx(
@@ -357,17 +370,19 @@ def tile_messagepassing_pa_kernel(tc, h, e, adj_mask, W_m1, b_m1, W_m2, b_m2, ou
             nc.vector.tensor_copy(
                 out=h_scales[:].bitcast(I32)[:, :, words : 2 * words], in_=h_scales[:].bitcast(I32)[:, :, 0:words]
             )
-        regroup_weights(XI_CHUNK + 1, 0, W1_VECTOR_COLS)
+        regroup_weights(XI_CHUNK + 1, 0, XI_VECTOR_COLS)
+        start_sum()
         quantise_weights(XI_CHUNK, 1, 0)
         quantise_weights(XI_CHUNK + 1, 1, 0)
         transpose_edges(0, range(4))
         target_products(0, 0, range(PACK))
-        regroup_weights(XJ_CHUNK, 0, XJ_VECTOR_COLS)
-        regroup_weights(XJ_CHUNK + 1, 0, XJ_VECTOR_COLS)
+        keep_tensor_busy()
+        regroup_weights(XJ_CHUNK, 0, EARLY_VECTOR_COLS)
+        regroup_weights(XJ_CHUNK + 1, 0, EARLY_VECTOR_COLS)
         quantise_edges(0)
-        regroup_weights(E2_CHUNK, 0, W1_VECTOR_COLS)
+        regroup_weights(E2_CHUNK, 0, EARLY_VECTOR_COLS)
         quantise_weights(XJ_CHUNK, 1, 0)
-        regroup_weights(E2_CHUNK + 1, 0, W1_VECTOR_COLS)
+        regroup_weights(E2_CHUNK + 1, 0, EARLY_VECTOR_COLS)
         quantise_weights(XJ_CHUNK + 1, 1, 0)
         transpose_edges(1, range(0, 2))
         source_term_products(0)
@@ -380,59 +395,55 @@ def tile_messagepassing_pa_kernel(tc, h, e, adj_mask, W_m1, b_m1, W_m2, b_m2, ou
 
         steps = [(g, c) for g in range(PASSES) for c in range(COL_TILES)]
         regroup_rounds = {
-            0: [(XI_CHUNK, 1), (XI_CHUNK + 1, 1)],
-            1: [(XJ_CHUNK, 1), (XJ_CHUNK + 1, 1), (E2_CHUNK, 1), (E2_CHUNK + 1, 1)],
+            0: [(XI_CHUNK, 1), (XI_CHUNK + 1, 1), (XJ_CHUNK, 1), (XJ_CHUNK + 1, 1)],
+            1: [(E2_CHUNK, 1), (E2_CHUNK + 1, 1)],
             2: [(M2_CHUNK, 0)],
             3: [(M2_CHUNK + 1, 0)],
             4: [(M2_CHUNK, 1)],
             5: [(M2_CHUNK + 1, 1)],
         }
+
+        def run(work_list, number):
+            for work, arguments in work_list[:number]:
+                work(*arguments)
+            return work_list[number:]
+
         to_multiply = []
         to_sum = []
         for n in range(len(steps) + QUANT_DELAY + 1):
-            if n == START_SUM_ROUND:
-                start_sum()
             vector_work = []
             if n + 1 < COL_TILES:
                 vector_work.append((quantise_edges, (n + 1,)))
+            scalar_work = []
+            if 0 <= n - RELU_DELAY < len(steps):
+                scalar_work.append((first_layer_relu, steps[n - RELU_DELAY]))
+            for chunk, half in regroup_rounds.get(n, []):
+                piece = (chunk, half, LATE_VECTOR_COLS if chunk < M2_CHUNK else M2_VECTOR_COLS)
+                scalar_work.append((regroup_scalar_share, piece))
+                vector_work.append((regroup_vector_share, piece))
             if 0 <= n - QUANT_DELAY < len(steps):
                 vector_work.append((quantise_hidden, steps[n - QUANT_DELAY]))
             for chunk, half in regroup_rounds.get(n - 1, []):
                 if chunk % PASSES == PASSES - 1:
                     vector_work.append((quantise_weights, (chunk - 1, PASSES, half)))
-            scalar_work = []
-            for chunk, half in regroup_rounds.get(n, []):
-                scalar_work.append((regroup_weights, (chunk, half, LATE_VECTOR_COLS if chunk < M2_CHUNK else 0)))
-            if 0 <= n - RELU_DELAY < len(steps):
-                scalar_work.insert(len(scalar_work) if n >= 2 else 0, (first_layer_relu, steps[n - RELU_DELAY]))
             if n == COL_TILES - 1:
-                work, arguments = scalar_work.pop(0)
-                work(*arguments)
                 source_term_products(1)
                 keep_source_term(1)
             for t in range(PACK):
                 if t % 2 == 0:
                     if n + 2 < COL_TILES:
-                        for number in range(n + 1 if t == 0 else 1):
-                            work, arguments = scalar_work.pop(0)
-                            work(*arguments)
+                        scalar_work = run(scalar_work, 1 if n == 0 else 0)
                         transpose_edges(n + 2, range(t, t + 2))
-                        for number in range(min(n, len(scalar_work))):
-                            work, arguments = scalar_work.pop(0)
-                            work(*arguments)
+                        scalar_work = run(scalar_work, n if t == 0 else len(scalar_work))
                     else:
-                        for number in range((len(scalar_work) + 1) // 2 if t == 0 else len(scalar_work)):
-                            work, arguments = scalar_work.pop(0)
-                            work(*arguments)
+                        scalar_work = run(scalar_work, (len(scalar_work) + 1) // 2 if t == 0 else len(scalar_work))
                 multiplied = to_multiply[:2]
                 to_multiply = to_multiply[2:]
                 for j, f in multiplied:
                     second_layer_products(j, f)
                 if n < len(steps):
                     first_layer_sum(steps[n][0], steps[n][1], t)
-                if vector_work:
-                    work, arguments = vector_work.pop(0)
-                    work(*arguments)
+                vector_work = run(vector_work, 1)
                 for j, f in to_sum:
                     second_layer_sum(j, f)
                 to_sum = multiplied
@@ -444,8 +455,7 @@ def tile_messagepassing_pa_kernel(tc, h, e, adj_mask, W_m1, b_m1, W_m2, b_m2, ou
                         edge_products(g, c, [t])
                     elif t == PACK - 1:
                         edge_products(g, c, range(PACK))
-            for work, arguments in vector_work:
-                work(*arguments)
+            run(vector_work, len(vector_work))
             if 0 <= n - QUANT_DELAY < len(steps):
                 g, c = steps[n - QUANT_DELAY]
                 if g == PASSES - 1:

@@ -33,12 +33,10 @@ RUN = 4
 
 XI_CHUNK, XJ_CHUNK, E2_CHUNK, M2_CHUNK = 0, 2, 4, 6
 WEIGHT_CHUNKS = 8
-XI_VECTOR_COLS = BANK // 4
-EARLY_VECTOR_COLS = 3 * BANK // 4
+EARLY_VECTOR_COLS = BANK // 4
 LATE_VECTOR_COLS = 3 * BANK // 8
-M2_VECTOR_COLS = BANK // 4
-IDLE_PRODUCTS = 4
-SIDE_NODE = 1
+M2_VECTOR_COLS = BANK // 2
+SIDE_NODE = 0
 RELU_DELAY, QUANT_DELAY = 2, 3
 
 FLOPS = 2 * WIDTH * WIDTH * (2 * NODES + 2 * EDGES)
@@ -298,11 +296,6 @@ def tile_messagepassing_pa_kernel(tc, h, e, adj_mask, W_m1, b_m1, W_m2, b_m2, ou
                 nc.tensor.matmul(out=b2_bank[:], lhsT=ones[:], rhs=b2_row[:, feats], start=True, stop=True)
                 nc.scalar.activation(out=side[:, feats], in_=b2_bank[:], func=COPY, scale=mask_sum[:, 0:1])
 
-        def keep_tensor_busy():
-            idle_bank = psum_short.tile([P, BANK], F32, name="idle_bank", tag="short")
-            for number in range(IDLE_PRODUCTS):
-                nc.tensor.matmul(out=idle_bank[:], lhsT=ones[:], rhs=b2_row[:, 0:BANK], start=True, stop=True)
-
         out_banks = {}
 
         def second_layer_products(j, f):
@@ -329,7 +322,7 @@ def tile_messagepassing_pa_kernel(tc, h, e, adj_mask, W_m1, b_m1, W_m2, b_m2, ou
                 nc.gpsimd.tensor_tensor(out=side[:, feats], in0=side[:, feats], in1=scaled[:], op=ADD)
                 return
             so_far = acc
-            if j == 0:
+            if j == SIDE_NODE + 1:
                 so_far = h_sb
             nc.vector.scalar_tensor_tensor(
                 out=acc[:, feats],
@@ -356,7 +349,7 @@ def tile_messagepassing_pa_kernel(tc, h, e, adj_mask, W_m1, b_m1, W_m2, b_m2, ou
             regroup_scalar_share(chunk, half, vector_cols)
             regroup_vector_share(chunk, half, vector_cols)
 
-        regroup_weights(XI_CHUNK, 0, XI_VECTOR_COLS)
+        regroup_weights(XI_CHUNK, 0, EARLY_VECTOR_COLS)
         nc.vector.tensor_copy(out=b1[:], in_=b1_bank[:, 0:BLOCKS])
         for g in range(PASSES):
             nc.vector.quantize_mx(
@@ -370,15 +363,14 @@ def tile_messagepassing_pa_kernel(tc, h, e, adj_mask, W_m1, b_m1, W_m2, b_m2, ou
             nc.vector.tensor_copy(
                 out=h_scales[:].bitcast(I32)[:, :, words : 2 * words], in_=h_scales[:].bitcast(I32)[:, :, 0:words]
             )
-        regroup_weights(XI_CHUNK + 1, 0, XI_VECTOR_COLS)
+        regroup_weights(XI_CHUNK + 1, 0, EARLY_VECTOR_COLS)
         start_sum()
         quantise_weights(XI_CHUNK, 1, 0)
         quantise_weights(XI_CHUNK + 1, 1, 0)
         transpose_edges(0, range(4))
         target_products(0, 0, range(PACK))
-        keep_tensor_busy()
-        regroup_weights(XJ_CHUNK, 0, EARLY_VECTOR_COLS)
-        regroup_weights(XJ_CHUNK + 1, 0, EARLY_VECTOR_COLS)
+        regroup_vector_share(XJ_CHUNK, 0, BANK)
+        regroup_vector_share(XJ_CHUNK + 1, 0, BANK)
         quantise_edges(0)
         regroup_weights(E2_CHUNK, 0, EARLY_VECTOR_COLS)
         quantise_weights(XJ_CHUNK, 1, 0)
@@ -415,26 +407,27 @@ def tile_messagepassing_pa_kernel(tc, h, e, adj_mask, W_m1, b_m1, W_m2, b_m2, ou
             if n + 1 < COL_TILES:
                 vector_work.append((quantise_edges, (n + 1,)))
             scalar_work = []
-            if 0 <= n - RELU_DELAY < len(steps):
-                scalar_work.append((first_layer_relu, steps[n - RELU_DELAY]))
             for chunk, half in regroup_rounds.get(n, []):
                 piece = (chunk, half, LATE_VECTOR_COLS if chunk < M2_CHUNK else M2_VECTOR_COLS)
                 scalar_work.append((regroup_scalar_share, piece))
                 vector_work.append((regroup_vector_share, piece))
+            if 0 <= n - RELU_DELAY < len(steps):
+                scalar_work.append((first_layer_relu, steps[n - RELU_DELAY]))
             if 0 <= n - QUANT_DELAY < len(steps):
                 vector_work.append((quantise_hidden, steps[n - QUANT_DELAY]))
             for chunk, half in regroup_rounds.get(n - 1, []):
                 if chunk % PASSES == PASSES - 1:
                     vector_work.append((quantise_weights, (chunk - 1, PASSES, half)))
             if n == COL_TILES - 1:
+                scalar_work = run(scalar_work, 1)
                 source_term_products(1)
                 keep_source_term(1)
             for t in range(PACK):
                 if t % 2 == 0:
                     if n + 2 < COL_TILES:
-                        scalar_work = run(scalar_work, 1 if n == 0 else 0)
+                        scalar_work = run(scalar_work, 1 if 2 * n == t else 0)
                         transpose_edges(n + 2, range(t, t + 2))
-                        scalar_work = run(scalar_work, n if t == 0 else len(scalar_work))
+                        scalar_work = run(scalar_work, 1 - n if t == 0 else len(scalar_work))
                     else:
                         scalar_work = run(scalar_work, (len(scalar_work) + 1) // 2 if t == 0 else len(scalar_work))
                 multiplied = to_multiply[:2]

@@ -36,6 +36,8 @@ WEIGHT_CHUNKS = 8
 EARLY_VECTOR_COLS = BANK // 4
 LATE_VECTOR_COLS = 3 * BANK // 8
 M2_VECTOR_COLS = BANK // 2
+GPSIMD_COLS = BANK // 4
+PAIR_STEPS = ((PASSES - 1, COL_TILES - 1),)
 SIDE_NODE = 0
 RELU_DELAY, QUANT_DELAY = 2, 3
 
@@ -151,6 +153,18 @@ def tile_messagepassing_pa_kernel(tc, h, e, adj_mask, W_m1, b_m1, W_m2, b_m2, ou
         def regroup_vector_share(chunk, half, vector_cols):
             regroup(nc.vector.tensor_copy, grouped_piece(chunk, half), raw_pieces[(chunk, half)], slice(0, vector_cols))
 
+        def regroup_on_gpsimd(chunk, half):
+            for first in range(0, BANK, GPSIMD_COLS):
+                cols = slice(first, first + GPSIMD_COLS)
+                nc.gpsimd.tensor_scalar(
+                    out=grouped_piece(chunk, half)[:, cols, :].rearrange("p (c i) t -> p c t i", i=RUN),
+                    in0=raw_pieces[(chunk, half)][:, :, cols].rearrange("p t (c i) -> p c t i", i=RUN),
+                    scalar1=1.0,
+                    scalar2=0.0,
+                    op0=MULT,
+                    op1=ADD,
+                )
+
         def quantise_weights(first_chunk, chunks, half):
             chunk_range = slice(first_chunk, first_chunk + chunks)
             members = slice(first_chunk % PASSES, first_chunk % PASSES + chunks)
@@ -165,8 +179,10 @@ def tile_messagepassing_pa_kernel(tc, h, e, adj_mask, W_m1, b_m1, W_m2, b_m2, ou
             nc.tensor.transpose(bank_cols, rows_bf16.bitcast(F32)[:, first : first + P], ident_f32[:])
 
         source_term = keep.tile([P, BLOCKS, NODES], F32)
+        target_term = keep.tile([P, PACK, NODES], F32)
         b1 = keep.tile([P, BLOCKS], F32)
         source_banks = {}
+        pair_terms = {}
 
         def source_term_products(half):
             bank = psum_short.tile([P, PACK, NODES], F32, name="source_bank", tag="short")
@@ -183,6 +199,39 @@ def tile_messagepassing_pa_kernel(tc, h, e, adj_mask, W_m1, b_m1, W_m2, b_m2, ou
                         stop=(kp == PASSES - 1),
                     )
             source_banks[half] = bank
+
+        def keep_target_term(half):
+            bank = psum_short.tile([P, PACK, NODES], F32, name="target_bank", tag="short")
+            for t in range(PACK):
+                units = slice(t * P, (t + 1) * P)
+                for kp in range(PASSES):
+                    nc.tensor.matmul_mx(
+                        out=bank[:, t, :],
+                        lhsT=w_codes[:, half, XI_CHUNK + kp, units].bitcast(FP8X4),
+                        lhsT_scale=w_scales[:, half, XI_CHUNK + kp, units],
+                        rhs=h_codes[:, kp, 0:NODES].bitcast(FP8X4),
+                        rhs_scale=h_scales[:, kp, 0:NODES],
+                        start=(kp == 0),
+                        stop=(kp == PASSES - 1),
+                    )
+            nc.scalar.copy(out=target_term[:], in_=bank[:])
+
+        def add_node_terms(g, c):
+            for t in range(PACK):
+                pair_term = stage.tile([P, BANK], F32, name="pair_term", tag="pair_term", bufs=4)
+                nc.gpsimd.tensor_tensor(
+                    out=pair_term[:].rearrange("p (j b i) -> p j b i", j=J_TILE, b=GRAPHS),
+                    in0=target_term[:, t, :]
+                    .rearrange("p (b i) -> p b i", b=GRAPHS)
+                    .unsqueeze(1)
+                    .to_broadcast([P, J_TILE, GRAPHS, GRAPH_NODES]),
+                    in1=source_term[:, PACK * g + t, :]
+                    .rearrange("p (b j) -> p j b", b=GRAPHS)[:, c * J_TILE : (c + 1) * J_TILE, :]
+                    .unsqueeze(3)
+                    .to_broadcast([P, J_TILE, GRAPHS, GRAPH_NODES]),
+                    op=ADD,
+                )
+                pair_terms[(g, c, t)] = pair_term
 
         def keep_source_term(half):
             for t in range(PACK):
@@ -222,6 +271,8 @@ def tile_messagepassing_pa_kernel(tc, h, e, adj_mask, W_m1, b_m1, W_m2, b_m2, ou
         r_grouped_tiles = {}
 
         def target_products(g, c, blocks):
+            if (g, c) in PAIR_STEPS:
+                return
             for t in blocks:
                 units = slice(t * P, (t + 1) * P)
                 edge_bank = psum.tile([P, BANK], F32, name="edge_bank", tag="bank")
@@ -238,8 +289,11 @@ def tile_messagepassing_pa_kernel(tc, h, e, adj_mask, W_m1, b_m1, W_m2, b_m2, ou
                 edge_banks[(g, c, t)] = edge_bank
 
         def edge_products(g, c, blocks):
+            alone = (g, c) in PAIR_STEPS
             for t in blocks:
                 units = slice(t * P, (t + 1) * P)
+                if alone:
+                    edge_banks[(g, c, t)] = psum.tile([P, BANK], F32, name="edge_bank", tag="bank")
                 for kp in range(PASSES):
                     nc.tensor.matmul_mx(
                         out=edge_banks[(g, c, t)][:],
@@ -247,13 +301,18 @@ def tile_messagepassing_pa_kernel(tc, h, e, adj_mask, W_m1, b_m1, W_m2, b_m2, ou
                         lhsT_scale=w_scales[:, g, E2_CHUNK + kp, units],
                         rhs=e_codes[:, c, kp, :].bitcast(FP8X4),
                         rhs_scale=e_scales[:, c, kp, :],
-                        start=False,
+                        start=(alone and kp == 0),
                         stop=(kp == PASSES - 1),
                     )
 
         def first_layer_sum(g, c, t):
             if t == 0:
                 p_tiles[(g, c)] = stage.tile([P, PACK, BANK], BF16, name="p_bf16", tag="p_bf16", bufs=4)
+            if (g, c) in PAIR_STEPS:
+                nc.vector.tensor_tensor(
+                    out=p_tiles[(g, c)][:, t, :], in0=edge_banks[(g, c, t)][:], in1=pair_terms[(g, c, t)][:], op=ADD
+                )
+                return
             nc.vector.tensor_tensor(
                 out=p_tiles[(g, c)][:, t, :].rearrange("p (j b i) -> p j b i", j=J_TILE, b=GRAPHS),
                 in0=edge_banks[(g, c, t)][:].rearrange("p (j b i) -> p j b i", j=J_TILE, b=GRAPHS),
@@ -391,8 +450,7 @@ def tile_messagepassing_pa_kernel(tc, h, e, adj_mask, W_m1, b_m1, W_m2, b_m2, ou
             1: [(E2_CHUNK, 1), (E2_CHUNK + 1, 1)],
             2: [(M2_CHUNK, 0)],
             3: [(M2_CHUNK + 1, 0)],
-            4: [(M2_CHUNK, 1)],
-            5: [(M2_CHUNK + 1, 1)],
+            5: [(M2_CHUNK, 1), (M2_CHUNK + 1, 1)],
         }
 
         def run(work_list, number):
@@ -407,7 +465,12 @@ def tile_messagepassing_pa_kernel(tc, h, e, adj_mask, W_m1, b_m1, W_m2, b_m2, ou
             if n + 1 < COL_TILES:
                 vector_work.append((quantise_edges, (n + 1,)))
             scalar_work = []
+            if n == COL_TILES - 1:
+                for chunk in range(M2_CHUNK, WEIGHT_CHUNKS):
+                    regroup_on_gpsimd(chunk, 1)
             for chunk, half in regroup_rounds.get(n, []):
+                if chunk >= M2_CHUNK and half == HALVES - 1:
+                    continue
                 piece = (chunk, half, LATE_VECTOR_COLS if chunk < M2_CHUNK else M2_VECTOR_COLS)
                 scalar_work.append((regroup_scalar_share, piece))
                 vector_work.append((regroup_vector_share, piece))
@@ -422,6 +485,9 @@ def tile_messagepassing_pa_kernel(tc, h, e, adj_mask, W_m1, b_m1, W_m2, b_m2, ou
                 scalar_work = run(scalar_work, 1)
                 source_term_products(1)
                 keep_source_term(1)
+                keep_target_term(1)
+                for g, c in PAIR_STEPS:
+                    add_node_terms(g, c)
             for t in range(PACK):
                 if t % 2 == 0:
                     if n + 2 < COL_TILES:

@@ -36,7 +36,6 @@ WEIGHT_CHUNKS = 8
 EARLY_VECTOR_COLS = BANK // 4
 LATE_VECTOR_COLS = 3 * BANK // 8
 M2_VECTOR_COLS = BANK // 2
-GPSIMD_COLS = BANK // 4
 PAIR_STEPS = ((PASSES - 1, COL_TILES - 1),)
 SIDE_NODE = 0
 RELU_DELAY, QUANT_DELAY = 2, 3
@@ -152,18 +151,6 @@ def tile_messagepassing_pa_kernel(tc, h, e, adj_mask, W_m1, b_m1, W_m2, b_m2, ou
 
         def regroup_vector_share(chunk, half, vector_cols):
             regroup(nc.vector.tensor_copy, grouped_piece(chunk, half), raw_pieces[(chunk, half)], slice(0, vector_cols))
-
-        def regroup_on_gpsimd(chunk, half):
-            for first in range(0, BANK, GPSIMD_COLS):
-                cols = slice(first, first + GPSIMD_COLS)
-                nc.gpsimd.tensor_scalar(
-                    out=grouped_piece(chunk, half)[:, cols, :].rearrange("p (c i) t -> p c t i", i=RUN),
-                    in0=raw_pieces[(chunk, half)][:, :, cols].rearrange("p t (c i) -> p c t i", i=RUN),
-                    scalar1=1.0,
-                    scalar2=0.0,
-                    op0=MULT,
-                    op1=ADD,
-                )
 
         def quantise_weights(first_chunk, chunks, half):
             chunk_range = slice(first_chunk, first_chunk + chunks)
@@ -450,7 +437,8 @@ def tile_messagepassing_pa_kernel(tc, h, e, adj_mask, W_m1, b_m1, W_m2, b_m2, ou
             1: [(E2_CHUNK, 1), (E2_CHUNK + 1, 1)],
             2: [(M2_CHUNK, 0)],
             3: [(M2_CHUNK + 1, 0)],
-            5: [(M2_CHUNK, 1), (M2_CHUNK + 1, 1)],
+            4: [(M2_CHUNK, 1)],
+            5: [(M2_CHUNK + 1, 1)],
         }
 
         def run(work_list, number):
@@ -465,12 +453,7 @@ def tile_messagepassing_pa_kernel(tc, h, e, adj_mask, W_m1, b_m1, W_m2, b_m2, ou
             if n + 1 < COL_TILES:
                 vector_work.append((quantise_edges, (n + 1,)))
             scalar_work = []
-            if n == COL_TILES - 1:
-                for chunk in range(M2_CHUNK, WEIGHT_CHUNKS):
-                    regroup_on_gpsimd(chunk, 1)
             for chunk, half in regroup_rounds.get(n, []):
-                if chunk >= M2_CHUNK and half == HALVES - 1:
-                    continue
                 piece = (chunk, half, LATE_VECTOR_COLS if chunk < M2_CHUNK else M2_VECTOR_COLS)
                 scalar_work.append((regroup_scalar_share, piece))
                 vector_work.append((regroup_vector_share, piece))

from contextlib import ExitStack

import concourse.mybir as mybir
from concourse.masks import make_identity

FP8X4 = mybir.dt.float8_e4m3fn_x4
BF16 = mybir.dt.bfloat16
F32 = mybir.dt.float32
U32 = mybir.dt.uint32
I32 = mybir.dt.int32
U8 = mybir.dt.uint8
ADD = mybir.AluOpType.add
MULT = mybir.AluOpType.mult
RELU = mybir.ActivationFunctionType.Relu
IDENTITY = mybir.ActivationFunctionType.Identity
COPY = mybir.ActivationFunctionType.Copy

P = 128
PACK = 4
K_PASS = P * PACK
BANK = 512
GRAPHS = 8
GRAPH_NODES = 16
NODES = GRAPHS * GRAPH_NODES
WIDTH = 1024
EDGES = NODES * GRAPH_NODES
PASSES = WIDTH // K_PASS
BLOCKS = WIDTH // P
J_TILE = BANK // NODES
COL_TILES = GRAPH_NODES // J_TILE
HALVES = WIDTH // BANK
RUN = 4

XI_CHUNK, XJ_CHUNK, E2_CHUNK, M2_CHUNK = 0, 2, 4, 6
WEIGHT_CHUNKS = 8
EARLY_VECTOR_COLS = BANK // 4
LATE_VECTOR_COLS = 3 * BANK // 8
M2_VECTOR_COLS = BANK // 2
PAIR_STEPS = ((PASSES - 1, COL_TILES - 1),)
SIDE_NODE = 0
RELU_DELAY, QUANT_DELAY = 2, 3

FLOPS = 2 * WIDTH * WIDTH * (2 * NODES + 2 * EDGES)


def tile_messagepassing_pa_kernel(tc, h, e, adj_mask, W_m1, b_m1, W_m2, b_m2, out):
    nc = tc.nc
    h_rows = h.rearrange("b i k -> (b i) k")
    e_rows = e.rearrange("b i j k -> (b i) j k")
    mask_rows = adj_mask.rearrange("b i j o -> (b i) (j o)")
    out_rows = out.rearrange("b i f -> (b i) f")

    with ExitStack() as stack:
        keep = stack.enter_context(tc.tile_pool(name="keep", bufs=1))
        raw_pool = stack.enter_context(tc.tile_pool(name="raw", bufs=6))
        edge_pool = stack.enter_context(tc.tile_pool(name="edge", bufs=3))
        grouped_pool = stack.enter_context(tc.tile_pool(name="grouped", bufs=3))
        stage = stack.enter_context(tc.tile_pool(name="stage", bufs=3))
        psum = stack.enter_context(tc.psum_pool(name="psum", bufs=5))
        psum_short = stack.enter_context(tc.psum_pool(name="psum_short", bufs=3))
        stack.enter_context(
            tc.manual_schedule(engines={mybir.EngineType.PE, mybir.EngineType.Activation, mybir.EngineType.DVE})
        )


        b1_rows = keep.tile([P, P], BF16)
        nc.vector.memset(b1_rows[:], 0.0)
        nc.scalar.dma_start(out=b1_rows[0:BLOCKS, :], in_=b_m1.rearrange("(m p) -> m p", p=P))
        mask_bf16 = keep.tile([P, GRAPH_NODES], BF16)
        nc.scalar.dma_start(out=mask_bf16[:], in_=mask_rows)
        b2_row = keep.tile([P, WIDTH], BF16)
        nc.gpsimd.memset(b2_row[:], 0.0)
        nc.scalar.dma_start(out=b2_row[0:1, :], in_=b_m2.rearrange("(o f) -> o f", o=1))

        h_sb = keep.tile([P, WIDTH], BF16)
        nc.sync.dma_start(out=h_sb[:], in_=h_rows)

        def load_w1_piece(chunk, half):
            raw = raw_pool.tile([P, PACK, BANK], BF16, name="raw", tag="raw")
            for u in range(2):
                first = chunk * K_PASS + 2 * P * u
                rows = W_m1[first : first + 2 * P, half * BANK : (half + 1) * BANK]
                nc.sync.dma_start(out=raw[:, 2 * u : 2 * u + 2, :], in_=rows.rearrange("(p s) n -> p s n", s=2))
            return raw

        def load_w2_piece(g, half):
            raw = raw_pool.tile([P, PACK, BANK], BF16, name="raw", tag="raw")
            rows = W_m2[g * K_PASS : (g + 1) * K_PASS, half * BANK : (half + 1) * BANK]
            nc.sync.dma_start(out=raw[:], in_=rows.rearrange("(t p) n -> p t n", t=PACK))
            return raw

        def load_edges(c):
            e_sb = edge_pool.tile([P, J_TILE, WIDTH], BF16, name="e_sb", tag="e_sb")
            nc.sync.dma_start(out=e_sb[:], in_=e_rows[:, c * J_TILE : (c + 1) * J_TILE, :])
            return e_sb

        raw_pieces = {}
        for chunk in range(XI_CHUNK, XJ_CHUNK):
            raw_pieces[(chunk, 0)] = load_w1_piece(chunk, 0)
        e_tiles = [load_edges(0)]
        for chunk in range(XJ_CHUNK, M2_CHUNK):
            raw_pieces[(chunk, 0)] = load_w1_piece(chunk, 0)
        e_tiles.extend([load_edges(c) for c in range(1, COL_TILES - 1)])
        for chunk in range(XI_CHUNK, E2_CHUNK):
            raw_pieces[(chunk, 1)] = load_w1_piece(chunk, 1)
        e_tiles.append(load_edges(COL_TILES - 1))
        for chunk in range(E2_CHUNK, M2_CHUNK):
            raw_pieces[(chunk, 1)] = load_w1_piece(chunk, 1)
        for half in range(HALVES):
            for g in range(PASSES):
                raw_pieces[(M2_CHUNK + g, half)] = load_w2_piece(g, half)

        warm = keep.tile([P, 1], F32)
        nc.vector.memset(warm[:], 0.0)
        nc.scalar.activation(out=warm[:], in_=warm[:], func=RELU)

        ident_f32 = keep.tile([P, P], F32)
        make_identity(nc, ident_f32[:])
        ident_bf16 = keep.tile([P, P], BF16)
        make_identity(nc, ident_bf16[:])
        ones = keep.tile([P, P], BF16)
        nc.vector.memset(ones[:], 1.0)

        w_codes = keep.tile([P, HALVES, WEIGHT_CHUNKS, BANK], U32, align_bytes=64)
        w_scales = keep.tile([P, HALVES, WEIGHT_CHUNKS, BANK], U8, align_bytes=64)
        h_codes = keep.tile([P, PASSES, BANK], U32, align_bytes=64)
        h_scales = keep.tile([P, PASSES, BANK], U8, align_bytes=64)
        e_codes = keep.tile([P, COL_TILES, PASSES, BANK], U32, align_bytes=64)
        e_scales = keep.tile([P, COL_TILES, PASSES, BANK], U8, align_bytes=64)
        r_codes = keep.tile([P, PASSES, EDGES], U32, align_bytes=64)
        r_scales = keep.tile([P, PASSES, EDGES], U8, align_bytes=64)

        def regroup(copy, grouped, raw, cols):
            copy(
                out=grouped[:, cols, :].rearrange("p (c i) t -> p c t i", i=RUN),
                in_=raw[:, :, cols].rearrange("p t (c i) -> p c t i", i=RUN),
            )

        grouped_pairs = {}

        def grouped_piece(chunk, half):
            pair, member = chunk // PASSES, chunk % PASSES
            if (pair, half) not in grouped_pairs:
                grouped_pairs[(pair, half)] = grouped_pool.tile(
                    [P, PASSES, BANK, PACK], BF16, name="grouped", tag="grouped", align_bytes=64
                )
            return grouped_pairs[(pair, half)][:, member, :, :]

        def regroup_scalar_share(chunk, half, vector_cols):
            regroup(nc.scalar.copy, grouped_piece(chunk, half), raw_pieces[(chunk, half)], slice(vector_cols, BANK))

        def regroup_vector_share(chunk, half, vector_cols):
            regroup(nc.vector.tensor_copy, grouped_piece(chunk, half), raw_pieces[(chunk, half)], slice(0, vector_cols))

        def quantise_weights(first_chunk, chunks, half):
            chunk_range = slice(first_chunk, first_chunk + chunks)
            members = slice(first_chunk % PASSES, first_chunk % PASSES + chunks)
            nc.vector.quantize_mx(
                out=w_codes[:, half, chunk_range, :].rearrange("p c n -> p (c n)").bitcast(FP8X4),
                scales=w_scales[:, half, chunk_range, :].rearrange("p c n -> p (c n)"),
                in_=grouped_pairs[(first_chunk // PASSES, half)][:, members, :, :].rearrange("p c n t -> p (c n t)"),
            )

        def transpose_words(bank_cols, rows_bf16, g, u):
            first = (K_PASS * g + 2 * P * u) // 2
            nc.tensor.transpose(bank_cols, rows_bf16.bitcast(F32)[:, first : first + P], ident_f32[:])

        source_term = keep.tile([P, BLOCKS, NODES], F32)
        target_term = keep.tile([P, PACK, NODES], F32)
        b1 = keep.tile([P, BLOCKS], F32)
        source_banks = {}
        pair_terms = {}

        def source_term_products(half):
            bank = psum_short.tile([P, PACK, NODES], F32, name="source_bank", tag="short")
            for t in range(PACK):
                units = slice(t * P, (t + 1) * P)
                for kp in range(PASSES):
                    nc.tensor.matmul_mx(
                        out=bank[:, t, :],
                        lhsT=w_codes[:, half, XJ_CHUNK + kp, units].bitcast(FP8X4),
                        lhsT_scale=w_scales[:, half, XJ_CHUNK + kp, units],
                        rhs=h_codes[:, kp, 0:NODES].bitcast(FP8X4),
                        rhs_scale=h_scales[:, kp, 0:NODES],
                        start=(kp == 0),
                        stop=(kp == PASSES - 1),
                    )
            source_banks[half] = bank

        def keep_target_term(half):
            bank = psum_short.tile([P, PACK, NODES], F32, name="target_bank", tag="short")
            for t in range(PACK):
                units = slice(t * P, (t + 1) * P)
                for kp in range(PASSES):
                    nc.tensor.matmul_mx(
                        out=bank[:, t, :],
                        lhsT=w_codes[:, half, XI_CHUNK + kp, units].bitcast(FP8X4),
                        lhsT_scale=w_scales[:, half, XI_CHUNK + kp, units],
                        rhs=h_codes[:, kp, 0:NODES].bitcast(FP8X4),
                        rhs_scale=h_scales[:, kp, 0:NODES],
                        start=(kp == 0),
                        stop=(kp == PASSES - 1),
                    )
            nc.scalar.copy(out=target_term[:], in_=bank[:])

        def add_node_terms(g, c):
            for t in range(PACK):
                pair_term = stage.tile([P, BANK], F32, name="pair_term", tag="pair_term", bufs=4)
                nc.gpsimd.tensor_tensor(
                    out=pair_term[:].rearrange("p (j b i) -> p j b i", j=J_TILE, b=GRAPHS),
                    in0=target_term[:, t, :]
                    .rearrange("p (b i) -> p b i", b=GRAPHS)
                    .unsqueeze(1)
                    .to_broadcast([P, J_TILE, GRAPHS, GRAPH_NODES]),
                    in1=source_term[:, PACK * g + t, :]
                    .rearrange("p (b j) -> p j b", b=GRAPHS)[:, c * J_TILE : (c + 1) * J_TILE, :]
                    .unsqueeze(3)
                    .to_broadcast([P, J_TILE, GRAPHS, GRAPH_NODES]),
                    op=ADD,
                )
                pair_terms[(g, c, t)] = pair_term

        def keep_source_term(half):
            for t in range(PACK):
                block = PACK * half + t
                nc.scalar.activation(
                    out=source_term[:, block, :], in_=source_banks[half][:, t, :], func=IDENTITY, bias=b1[:, block : block + 1]
                )

        e_grouped_tiles = {}

        def transpose_edges(c, banks):
            for number in banks:
                g, first_j = number // 2, 2 * (number % 2)
                if number == 0:
                    e_grouped_tiles[c] = stage.tile(
                        [P, PASSES, BANK * PACK], BF16, name="e_grouped", tag="e_grouped", bufs=2, align_bytes=64
                    )
                e_words = e_grouped_tiles[c][:, g, :].bitcast(F32).rearrange("p (x n u) -> p x n u", x=J_TILE, u=2)
                e_bank = psum_short.tile([P, 2, 2, NODES], F32, name="e_bank", tag="short")
                for x in range(2):
                    for u in range(2):
                        transpose_words(e_bank[:, x, u, :], e_tiles[c][:, first_j + x, :], g, u)
                nc.scalar.copy(
                    out=e_words[:, first_j : first_j + 2, :, :],
                    in_=e_bank[:].rearrange("p x u n -> p x n u"),
                )

        def quantise_edges(c):
            nc.vector.quantize_mx(
                out=e_codes[:, c, :, :].rearrange("p g n -> p (g n)").bitcast(FP8X4),
                scales=e_scales[:, c, :, :].rearrange("p g n -> p (g n)"),
                in_=e_grouped_tiles[c][:].rearrange("p g k -> p (g k)"),
            )

        edge_banks = {}
        p_tiles = {}
        r_grouped_tiles = {}

        def target_products(g, c, blocks):
            if (g, c) in PAIR_STEPS:
                return
            for t in blocks:
                units = slice(t * P, (t + 1) * P)
                edge_bank = psum.tile([P, BANK], F32, name="edge_bank", tag="bank")
                for kp in range(PASSES):
                    nc.tensor.matmul_mx(
                        out=edge_bank[:],
                        lhsT=w_codes[:, g, XI_CHUNK + kp, units].bitcast(FP8X4),
                        lhsT_scale=w_scales[:, g, XI_CHUNK + kp, units],
                        rhs=h_codes[:, kp, :].bitcast(FP8X4),
                        rhs_scale=h_scales[:, kp, :],
                        start=(kp == 0),
                        stop=False,
                    )
                edge_banks[(g, c, t)] = edge_bank

        def edge_products(g, c, blocks):
            alone = (g, c) in PAIR_STEPS
            for t in blocks:
                units = slice(t * P, (t + 1) * P)
                if alone:
                    edge_banks[(g, c, t)] = psum.tile([P, BANK], F32, name="edge_bank", tag="bank")
                for kp in range(PASSES):
                    nc.tensor.matmul_mx(
                        out=edge_banks[(g, c, t)][:],
                        lhsT=w_codes[:, g, E2_CHUNK + kp, units].bitcast(FP8X4),
                        lhsT_scale=w_scales[:, g, E2_CHUNK + kp, units],
                        rhs=e_codes[:, c, kp, :].bitcast(FP8X4),
                        rhs_scale=e_scales[:, c, kp, :],
                        start=(alone and kp == 0),
                        stop=(kp == PASSES - 1),
                    )

        def first_layer_sum(g, c, t):
            if t == 0:
                p_tiles[(g, c)] = stage.tile([P, PACK, BANK], BF16, name="p_bf16", tag="p_bf16", bufs=4)
            if (g, c) in PAIR_STEPS:
                nc.vector.tensor_tensor(
                    out=p_tiles[(g, c)][:, t, :], in0=edge_banks[(g, c, t)][:], in1=pair_terms[(g, c, t)][:], op=ADD
                )
                return
            nc.vector.tensor_tensor(
                out=p_tiles[(g, c)][:, t, :].rearrange("p (j b i) -> p j b i", j=J_TILE, b=GRAPHS),
                in0=edge_banks[(g, c, t)][:].rearrange("p (j b i) -> p j b i", j=J_TILE, b=GRAPHS),
                in1=source_term[:, PACK * g + t, :]
                .rearrange("p (b j) -> p j b", b=GRAPHS)[:, c * J_TILE : (c + 1) * J_TILE, :]
                .unsqueeze(3)
                .to_broadcast([P, J_TILE, GRAPHS, GRAPH_NODES]),
                op=ADD,
            )

        def first_layer_relu(g, c):
            r_grouped = stage.tile([P, BANK, PACK], BF16, name="r_grouped", tag="r_grouped", align_bytes=64)
            nc.scalar.activation(
                out=r_grouped[:].rearrange("p (c i) t -> p c t i", i=RUN),
                in_=p_tiles[(g, c)][:].rearrange("p t (c i) -> p c t i", i=RUN),
                func=RELU,
            )
            r_grouped_tiles[(g, c)] = r_grouped

        def quantise_hidden(g, c):
            cols = slice(c * BANK, (c + 1) * BANK)
            nc.vector.quantize_mx(
                out=r_codes[:, g, cols].bitcast(FP8X4),
                scales=r_scales[:, g, cols],
                in_=r_grouped_tiles[(g, c)][:].rearrange("p c t -> p (c t)"),
            )

        mask = keep.tile([P, GRAPH_NODES], F32)
        mask_sum = keep.tile([P, 1], F32)
        acc = keep.tile([P, WIDTH], F32)
        side = keep.tile([P, WIDTH], F32)
        scaled_pool = stack.enter_context(tc.tile_pool(name="scaled", bufs=3))
        nc.vector.tensor_copy(out=mask[:], in_=mask_bf16[:])
        nc.vector.tensor_reduce(out=mask_sum[:], in_=mask[:], axis=mybir.AxisListType.X, op=ADD)

        def start_sum():
            for f in range(HALVES):
                feats = slice(f * BANK, (f + 1) * BANK)
                b2_bank = psum_short.tile([P, BANK], F32, name="b2_bank", tag="short")
                nc.tensor.matmul(out=b2_bank[:], lhsT=ones[:], rhs=b2_row[:, feats], start=True, stop=True)
                nc.scalar.activation(out=side[:, feats], in_=b2_bank[:], func=COPY, scale=mask_sum[:, 0:1])

        out_banks = {}

        def second_layer_products(j, f):
            nodes = slice(j * NODES, (j + 1) * NODES)
            out_bank = psum.tile([P, BANK], F32, name="out_bank", tag="bank")
            for g in range(PASSES):
                nc.tensor.matmul_mx(
                    out=out_bank[:],
                    lhsT=r_codes[:, g, nodes].bitcast(FP8X4),
                    lhsT_scale=r_scales[:, g, nodes],
                    rhs=w_codes[:, f, M2_CHUNK + g, :].bitcast(FP8X4),
                    rhs_scale=w_scales[:, f, M2_CHUNK + g, :],
                    start=(g == 0),
                    stop=(g == PASSES - 1),
                )
            out_banks[(j, f)] = out_bank

        def second_layer_sum(j, f):
            feats = slice(f * BANK, (f + 1) * BANK)
            c, x = j // J_TILE, j % J_TILE
            if x == SIDE_NODE:
                scaled = scaled_pool.tile([P, BANK], F32, name="scaled", tag="scaled")
                nc.scalar.activation(out=scaled[:], in_=out_banks[(j, f)][:], func=COPY, scale=mask[:, j : j + 1])
                nc.gpsimd.tensor_tensor(out=side[:, feats], in0=side[:, feats], in1=scaled[:], op=ADD)
                return
            so_far = acc
            if j == SIDE_NODE + 1:
                so_far = h_sb
            nc.vector.scalar_tensor_tensor(
                out=acc[:, feats],
                in0=out_banks[(j, f)][:],
                scalar=mask[:, j : j + 1],
                in1=so_far[:, feats],
                op0=MULT,
                op1=ADD,
            )

        h_bank = psum_short.tile([P, PASSES, 2, NODES], F32, name="h_bank", tag="short")
        for g in range(PASSES):
            for u in range(2):
                transpose_words(h_bank[:, g, u, :], h_sb[:], g, u)
        h_grouped = keep.tile([P, PASSES, NODES * PACK], BF16, align_bytes=64)
        nc.scalar.copy(
            out=h_grouped[:].rearrange("p g k -> p (g k)").bitcast(F32).rearrange("p (g n u) -> p g n u", g=PASSES, u=2),
            in_=h_bank[:].rearrange("p g u n -> p g n u"),
        )
        b1_bank = psum_short.tile([P, P], BF16, name="b1_bank", tag="short")
        nc.tensor.transpose(b1_bank[:], b1_rows[:], ident_bf16[:])

        def regroup_weights(chunk, half, vector_cols):
            regroup_scalar_share(chunk, half, vector_cols)
            regroup_vector_share(chunk, half, vector_cols)

        regroup_weights(XI_CHUNK, 0, EARLY_VECTOR_COLS)
        nc.vector.tensor_copy(out=b1[:], in_=b1_bank[:, 0:BLOCKS])
        for g in range(PASSES):
            nc.vector.quantize_mx(
                out=h_codes[:, g, 0:NODES].bitcast(FP8X4), scales=h_scales[:, g, 0:NODES], in_=h_grouped[:, g, :]
            )
        for width in (NODES, 2 * NODES):
            nc.vector.tensor_copy(
                out=h_codes[:].bitcast(I32)[:, :, width : 2 * width], in_=h_codes[:].bitcast(I32)[:, :, 0:width]
            )
            words = width // PACK
            nc.vector.tensor_copy(
                out=h_scales[:].bitcast(I32)[:, :, words : 2 * words], in_=h_scales[:].bitcast(I32)[:, :, 0:words]
            )
        regroup_weights(XI_CHUNK + 1, 0, EARLY_VECTOR_COLS)
        start_sum()
        quantise_weights(XI_CHUNK, 1, 0)
        quantise_weights(XI_CHUNK + 1, 1, 0)
        transpose_edges(0, range(4))
        target_products(0, 0, range(PACK))
        regroup_vector_share(XJ_CHUNK, 0, BANK)
        regroup_vector_share(XJ_CHUNK + 1, 0, BANK)
        quantise_edges(0)
        regroup_weights(E2_CHUNK, 0, EARLY_VECTOR_COLS)
        quantise_weights(XJ_CHUNK, 1, 0)
        regroup_weights(E2_CHUNK + 1, 0, EARLY_VECTOR_COLS)
        quantise_weights(XJ_CHUNK + 1, 1, 0)
        transpose_edges(1, range(0, 2))
        source_term_products(0)
        keep_source_term(0)
        transpose_edges(1, range(2, 4))
        quantise_weights(E2_CHUNK, 1, 0)
        quantise_weights(E2_CHUNK + 1, 1, 0)
        edge_products(0, 0, range(PACK))
        target_products(0, 1, range(0, 1))

        steps = [(g, c) for g in range(PASSES) for c in range(COL_TILES)]
        regroup_rounds = {
            0: [(XI_CHUNK, 1), (XI_CHUNK + 1, 1), (XJ_CHUNK, 1), (XJ_CHUNK + 1, 1)],
            1: [(E2_CHUNK, 1), (E2_CHUNK + 1, 1)],
            2: [(M2_CHUNK, 0)],
            3: [(M2_CHUNK + 1, 0)],
            4: [(M2_CHUNK, 1)],
            5: [(M2_CHUNK + 1, 1)],
        }

        def run(work_list, number):
            for work, arguments in work_list[:number]:
                work(*arguments)
            return work_list[number:]

        to_multiply = []
        to_sum = []
        for n in range(len(steps) + QUANT_DELAY + 1):
            vector_work = []
            if n + 1 < COL_TILES:
                vector_work.append((quantise_edges, (n + 1,)))
            scalar_work = []
            for chunk, half in regroup_rounds.get(n, []):
                piece = (chunk, half, LATE_VECTOR_COLS if chunk < M2_CHUNK else M2_VECTOR_COLS)
                scalar_work.append((regroup_scalar_share, piece))
                vector_work.append((regroup_vector_share, piece))
            if 0 <= n - RELU_DELAY < len(steps):
                scalar_work.append((first_layer_relu, steps[n - RELU_DELAY]))
            if 0 <= n - QUANT_DELAY < len(steps):
                vector_work.append((quantise_hidden, steps[n - QUANT_DELAY]))
            for chunk, half in regroup_rounds.get(n - 1, []):
                if chunk % PASSES == PASSES - 1:
                    vector_work.append((quantise_weights, (chunk - 1, PASSES, half)))
            if n == COL_TILES - 1:
                scalar_work = run(scalar_work, 1)
                source_term_products(1)
                keep_source_term(1)
                keep_target_term(1)
                for g, c in PAIR_STEPS:
                    add_node_terms(g, c)
            for t in range(PACK):
                if t % 2 == 0:
                    if n + 2 < COL_TILES:
                        scalar_work = run(scalar_work, 1 if 2 * n == t else 0)
                        transpose_edges(n + 2, range(t, t + 2))
                        scalar_work = run(scalar_work, 1 - n if t == 0 else len(scalar_work))
                    else:
                        scalar_work = run(scalar_work, (len(scalar_work) + 1) // 2 if t == 0 else len(scalar_work))
                multiplied = to_multiply[:2]
                to_multiply = to_multiply[2:]
                for j, f in multiplied:
                    second_layer_products(j, f)
                if n < len(steps):
                    first_layer_sum(steps[n][0], steps[n][1], t)
                vector_work = run(vector_work, 1)
                for j, f in to_sum:
                    second_layer_sum(j, f)
                to_sum = multiplied
                if n + 1 < len(steps):
                    g, c = steps[n + 1]
                    if n > 0 or t >= 1:
                        target_products(g, c, [t])
                    if n > 0:
                        edge_products(g, c, [t])
                    elif t == PACK - 1:
                        edge_products(g, c, range(PACK))
            run(vector_work, len(vector_work))
            if 0 <= n - QUANT_DELAY < len(steps):
                g, c = steps[n - QUANT_DELAY]
                if g == PASSES - 1:
                    to_multiply.extend([(j, f) for j in range(c * J_TILE, (c + 1) * J_TILE) for f in range(HALVES)])
        for j, f in to_sum:
            second_layer_sum(j, f)

        for f in range(HALVES):
            feats = slice(f * BANK, (f + 1) * BANK)
            nc.vector.tensor_tensor(out=acc[:, feats], in0=acc[:, feats], in1=side[:, feats], op=ADD)
            nc.sync.dma_start(out=out_rows[:, feats], in_=acc[:, feats])
